import numpy as np
import ml_dtypes


def mxq(x, axis, fmt="e4m3"):
    dtype, down = {"e4m3": (ml_dtypes.float8_e4m3fn, 7), "e5m2": (ml_dtypes.float8_e5m2, 14)}[fmt]
    v = np.moveaxis(np.asarray(x, np.float32).astype(ml_dtypes.bfloat16).astype(np.float64), axis, -1)
    blocks = v.reshape(v.shape[:-1] + (-1, 32))
    amax = np.abs(blocks).max(-1, keepdims=True)
    byte = np.maximum(np.where(amax > 0, np.frexp(amax)[1] - 1 + 127, 0) - down, 1)
    scale = np.exp2(byte - 127.0)
    codes = (blocks / scale).astype(np.float32).astype(dtype).astype(np.float64)
    return np.moveaxis((codes * scale).reshape(v.shape), -1, axis)


WIDE = False


def mx_kscale(k):
    if not WIDE:
        return np.ones(k)
    levels = np.array([10, -10, 5, -5, 0])
    a = np.random.permutation(np.resize(levels, k // 512 * 4)).reshape(k // 512, 4)
    idx = np.arange(k)
    return np.exp2(a[idx // 512, idx % 128 // 32])


BF16 = ml_dtypes.bfloat16


def bf(x):
    return np.asarray(x, np.float32).astype(BF16)


def f64(x):
    return np.asarray(x).astype(np.float64)


B, S, D, A0, A1, A2 = 4, 1024, 1024, 32, 16, 64
AM = min(A0, A1, A2)


def kron(a, b):
    return (a[:, None, :, None] * b[None, :, None, :]).reshape(a.shape[0] * b.shape[0], a.shape[1] * b.shape[1])


def setup_inputs():
    u = mx_kscale(D)[:: D // AM]
    s = np.repeat(u, D // AM)
    inp = {"x": bf(np.random.standard_normal((B, S, D)) * s)}
    for i, a in enumerate((A0, A1, A2)):
        inp[f"L{i}"] = bf(np.random.uniform(size=(a, a)) / np.repeat(u, a // AM)[:, None])
        inp[f"R{i}"] = bf(np.random.uniform(size=(D // a, D // a)) * 3.0 / np.sqrt(D))
    inp["bias"] = bf(np.random.uniform(size=D))
    return inp


def reference(x, L0, R0, L1, R1, L2, R2, bias):
    pairs = [(f64(L0), f64(R0)), (f64(L1), f64(R1)), (f64(L2), f64(R2))]
    W = kron(pairs[0][0], pairs[0][1])
    for l, r in pairs[1:]:
        W = W + kron(l, r)
    W = W / len(pairs)
    return (mxq(f64(x), 2, "e4m3") @ mxq(W, 0, "e4m3")) + f64(bias)

@@ -1,0 +1,185 @@
+from contextlib import ExitStack
+
+import concourse.mybir as mybir
+from concourse.masks import make_identity
+
+F32 = mybir.dt.float32
+BF16 = mybir.dt.bfloat16
+U32 = mybir.dt.uint32
+U8 = mybir.dt.uint8
+FP8X4 = mybir.dt.float8_e4m3fn_x4
+MULT = mybir.AluOpType.mult
+ADD = mybir.AluOpType.add
+
+P = 128
+D = 1024
+TOKENS = 4096
+FLOPS = 2 * TOKENS * D * D
+PINNED = True
+N_MACRO = 16
+
+
+def tile_klinear_t_kernel(tc, x, L0, R0, L1, R1, L2, R2, bias, out):
+    nc = tc.nc
+    terms = [(L1, R1, 16, 64), (L0, R0, 32, 32), (L2, R2, 64, 16)]
+    r_off = [0, 256, 384]
+    l_off = [0, 32, 96]
+    xv = x.flatten_outer_dims().rearrange("(m p j) k -> m p (j k)", p=P, j=2)
+    ov = out.flatten_outer_dims().rearrange("(m p j) n -> m p (j n)", p=P, j=2)
+
+    with ExitStack() as ctx:
+        keep = ctx.enter_context(tc.tile_pool(name="keep", bufs=1))
+        xpool = ctx.enter_context(tc.tile_pool(name="xpool", bufs=4))
+        opool = ctx.enter_context(tc.tile_pool(name="opool", bufs=4))
+        psum = ctx.enter_context(tc.psum_pool(name="psum", bufs=8))
+        if PINNED:
+            ctx.enter_context(tc.manual_schedule())
+
+        raw = keep.tile([P, 768], BF16)
+        rawb = keep.tile([P, D], BF16)
+        ident = keep.tile([P, P], F32)
+        sel1 = keep.tile([P, P], BF16)
+        sel2 = keep.tile([P, P], BF16)
+        rrow = keep.tile([P, 448], F32)
+        lrow = keep.tile([P, 224], F32)
+        bias_sb = keep.tile([P, D], F32)
+        acc = keep.tile([P, 2, 4 * D], F32)
+        wbf = keep.tile([P, 2, 4 * D], BF16, align_bytes=64)
+        wc = keep.tile([P, 2, D], U32, align_bytes=64)
+        ws = keep.tile([P, 2, D], U8, align_bytes=64)
+        xg = keep.tile([P, N_MACRO, 2048], BF16, align_bytes=64)
+        xc = keep.tile([P, N_MACRO, 512], U32, align_bytes=64)
+        xs = keep.tile([P, N_MACRO, 512], U8, align_bytes=64)
+
+        nc.vector.memset(raw[:].bitcast(F32), 0.0)
+        make_identity(nc, ident[:])
+        for s, (lm, rm, np_, r) in enumerate(terms):
+            nq = r // 4
+            nc.sync.dma_start(
+                out=raw[32 * s : 32 * s + nq, r_off[s] : r_off[s] + 4 * r],
+                in_=rm.rearrange("(q t) d -> q (t d)", t=4),
+            )
+        for s, (lm, rm, np_, r) in enumerate(terms):
+            ns = 512 // r
+            nc.sync.dma_start(
+                out=raw[32 * s : 32 * s + ns, 512 + l_off[s] : 512 + l_off[s] + 2 * np_].rearrange(
+                    "s (g b) -> s g b", g=2
+                ),
+                in_=lm.rearrange("(g s) b -> s g b", g=2),
+            )
+        nc.vector.memset(rawb[:].bitcast(F32), 0.0)
+        nc.sync.dma_start(out=rawb[96:97, :], in_=bias.unsqueeze(0))
+
+        for s, (lm, rm, np_, r) in enumerate(terms):
+            nq = r // 4
+            ns = 512 // r
+            rows = slice(32 * s, 32 * s + 32)
+            nc.vector.tensor_copy(
+                out=sel1[rows, :].rearrange("k (a b) -> k a b", b=nq),
+                in_=ident[rows, 32 * s : 32 * s + nq].unsqueeze(1).to_broadcast([32, P // nq, nq]),
+            )
+            nc.vector.tensor_copy(
+                out=sel2[rows, :].rearrange("k (a b) -> k a b", b=nq),
+                in_=ident[rows, 32 * s : 32 * s + ns].unsqueeze(2).to_broadcast([32, ns, nq]),
+            )
+        nc.vector.tensor_copy(out=sel1[96:128, :], in_=ident[96:128, 96:97].to_broadcast([32, P]))
+        nc.vector.memset(sel2[96:128, :], 0.0)
+
+        bank_r = psum.tile([P, 512], F32, tag="bank")
+        nc.tensor.matmul(out=bank_r[:], lhsT=sel1[:], rhs=raw[:, 0:512], start=True, stop=True)
+        bank_l = psum.tile([P, 512], F32, tag="bank")
+        nc.tensor.matmul(out=bank_l[:, 0:256], lhsT=sel2[:], rhs=raw[:, 512:768], start=True, stop=True)
+        nc.vector.tensor_scalar(
+            out=lrow[:], in0=bank_l[:, 0:224], scalar1=1.0 / 3.0, scalar2=None, op0=MULT
+        )
+        for s, (lm, rm, np_, r) in enumerate(terms):
+            cols = slice(r_off[s], r_off[s] + 4 * r)
+            nc.vector.tensor_copy(
+                out=rrow[:, cols].rearrange("p (d t) -> p d t", t=4),
+                in_=bank_r[:, cols].rearrange("p (t d) -> p d t", t=4),
+            )
+        for h in range(2):
+            bank_b = psum.tile([P, 512], F32, tag="bank")
+            nc.tensor.matmul(
+                out=bank_b[:], lhsT=sel1[:], rhs=rawb[:, 512 * h : 512 * h + 512], start=True, stop=True
+            )
+            nc.scalar.copy(out=bias_sb[:, 512 * h : 512 * h + 512], in_=bank_b[:])
+
+        for m in range(N_MACRO):
+            xr = xpool.tile([P, 2048], BF16, tag="xr")
+            nc.sync.dma_start(out=xr[:], in_=xv[m])
+            xw = xr[:].bitcast(F32)
+            xgw = xg[:, m, :].bitcast(F32)
+            for j in range(2):
+                xt = psum.tile([P, 4, P], F32, tag="bank")
+                for g in range(2):
+                    words = xw[:, 512 * j + 256 * g : 512 * j + 256 * g + 256].rearrange(
+                        "m (p u) -> m u p", u=2
+                    )
+                    for u in range(2):
+                        nc.tensor.transpose(xt[:, 2 * g + u, :], words[:, u, :], ident[:])
+                nc.scalar.copy(
+                    out=xgw[:, 512 * j : 512 * j + 512].rearrange("p (g m u) -> p g m u", g=2, u=2),
+                    in_=xt[:].rearrange("p (g u) m -> p g m u", u=2),
+                )
+
+        def w_term(s, g):
+            lm, rm, np_, r = terms[s]
+            w = 4 * r
+            rr = rrow[:, r_off[s] : r_off[s] + w]
+            for b in range(np_):
+                sc = lrow[:, l_off[s] + g * np_ + b : l_off[s] + g * np_ + b + 1]
+                dst = acc[:, g, w * b : w * b + w]
+                if s == 0:
+                    nc.vector.tensor_scalar(out=dst, in0=rr, scalar1=sc, scalar2=None, op0=MULT)
+                elif s == 1:
+                    nc.vector.scalar_tensor_tensor(out=dst, in0=rr, scalar=sc, in1=dst, op0=MULT, op1=ADD)
+                else:
+                    nc.vector.scalar_tensor_tensor(
+                        out=wbf[:, g, w * b : w * b + w], in0=rr, scalar=sc, in1=dst, op0=MULT, op1=ADD
+                    )
+
+        def w_quant(g):
+            nc.vector.quantize_mx(out=wc[:, g, :].bitcast(FP8X4), scales=ws[:, g, :], in_=wbf[:, g, :])
+
+        def x_quant(m):
+            nc.vector.quantize_mx(out=xc[:, m, :].bitcast(FP8X4), scales=xs[:, m, :], in_=xg[:, m, :])
+
+        w_term(0, 0)
+        w_term(1, 0)
+        w_term(2, 0)
+        w_term(0, 1)
+        w_quant(0)
+        w_term(1, 1)
+        w_term(2, 1)
+        x_quant(0)
+        w_quant(1)
+        x_quant(1)
+
+        for m in range(N_MACRO):
+            ot = opool.tile([P, 2 * D], F32, tag="ot")
+            n_sg = 1 + (m % 2)
+            for j in range(2):
+                for h in range(2):
+                    pb = psum.tile([P, 512], F32, tag="bank")
+                    for g in range(2):
+                        cols = slice(256 * j + 128 * g, 256 * j + 128 * g + 128)
+                        nc.tensor.matmul_mx(
+                            out=pb[:],
+                            lhsT=xc[:, m, cols].bitcast(FP8X4),
+                            lhsT_scale=xs[:, m, cols],
+                            rhs=wc[:, g, 512 * h : 512 * h + 512].bitcast(FP8X4),
+                            rhs_scale=ws[:, g, 512 * h : 512 * h + 512],
+                            start=(g == 0),
+                            stop=(g == 1),
+                        )
+                    dst = ot[:, D * j + 512 * h : D * j + 512 * h + 512]
+                    bs = bias_sb[:, 512 * h : 512 * h + 512]
+                    if 2 * j + h >= 4 - n_sg:
+                        nc.scalar.copy(out=dst, in_=pb[:])
+                        nc.gpsimd.tensor_tensor(out=dst, in0=dst, in1=bs, op=ADD)
+                    else:
+                        nc.vector.tensor_tensor(out=dst, in0=pb[:], in1=bs, op=ADD)
+            if m + 2 < N_MACRO:
+                x_quant(m + 2)
+            nc.sync.dma_start(out=ov[m], in_=ot[:])

@@ -15,8 +15,12 @@ P = 128
 D = 1024
 TOKENS = 4096
 FLOPS = 2 * TOKENS * D * D
-PINNED = True
 N_MACRO = 16
+EARLY = 6
+PRE_T = 12
+LATE_SG = [1, 2, 1, 2, 1, 2, 1, 2, 1, 1]
+BURSTS = {-2: [3], -1: [4], 6: [5, 6], 10: [7]}
+G_T1 = [(0, 1), (1, 0), (1, 1)]
 
 
 def tile_klinear_t_kernel(tc, x, L0, R0, L1, R1, L2, R2, bias, out):
@@ -26,30 +30,32 @@ def tile_klinear_t_kernel(tc, x, L0, R0, L1, R1, L2, R2, bias, out):
     l_off = [0, 32, 96]
     xv = x.flatten_outer_dims().rearrange("(m p j) k -> m p (j k)", p=P, j=2)
     ov = out.flatten_outer_dims().rearrange("(m p j) n -> m p (j n)", p=P, j=2)
+    ov3 = out.flatten_outer_dims().rearrange("(m p j) n -> m p j n", p=P, j=2)
 
     with ExitStack() as ctx:
         keep = ctx.enter_context(tc.tile_pool(name="keep", bufs=1))
         xpool = ctx.enter_context(tc.tile_pool(name="xpool", bufs=4))
-        opool = ctx.enter_context(tc.tile_pool(name="opool", bufs=4))
-        psum = ctx.enter_context(tc.psum_pool(name="psum", bufs=8))
-        if PINNED:
-            ctx.enter_context(tc.manual_schedule())
+        opool = ctx.enter_context(tc.tile_pool(name="opool", bufs=3))
+        hpool = ctx.enter_context(tc.tile_pool(name="hpool", bufs=4))
+        psum_r = ctx.enter_context(tc.psum_pool(name="psum_r", bufs=1))
+        psum = ctx.enter_context(tc.psum_pool(name="psum", bufs=7))
+        ctx.enter_context(tc.manual_schedule())
 
         raw = keep.tile([P, 768], BF16)
         rawb = keep.tile([P, D], BF16)
         ident = keep.tile([P, P], F32)
         sel1 = keep.tile([P, P], BF16)
         sel2 = keep.tile([P, P], BF16)
-        rrow = keep.tile([P, 448], F32)
+        rrow1 = keep.tile([P, 256], F32)
         lrow = keep.tile([P, 224], F32)
         bias_sb = keep.tile([P, D], F32)
         acc = keep.tile([P, 2, 4 * D], F32)
         wbf = keep.tile([P, 2, 4 * D], BF16, align_bytes=64)
         wc = keep.tile([P, 2, D], U32, align_bytes=64)
         ws = keep.tile([P, 2, D], U8, align_bytes=64)
-        xg = keep.tile([P, N_MACRO, 2048], BF16, align_bytes=64)
-        xc = keep.tile([P, N_MACRO, 512], U32, align_bytes=64)
-        xs = keep.tile([P, N_MACRO, 512], U8, align_bytes=64)
+        xg = keep.tile([P, N_MACRO * 2048], BF16, align_bytes=64)
+        xc = keep.tile([P, N_MACRO * 512], U32, align_bytes=64)
+        xs = keep.tile([P, N_MACRO * 512], U8, align_bytes=64)
 
         nc.vector.memset(raw[:].bitcast(F32), 0.0)
         make_identity(nc, ident[:])
@@ -85,19 +91,17 @@ def tile_klinear_t_kernel(tc, x, L0, R0, L1, R1, L2, R2, bias, out):
         nc.vector.tensor_copy(out=sel1[96:128, :], in_=ident[96:128, 96:97].to_broadcast([32, P]))
         nc.vector.memset(sel2[96:128, :], 0.0)
 
-        bank_r = psum.tile([P, 512], F32, tag="bank")
+        bank_r = psum_r.tile([P, 512], F32)
         nc.tensor.matmul(out=bank_r[:], lhsT=sel1[:], rhs=raw[:, 0:512], start=True, stop=True)
         bank_l = psum.tile([P, 512], F32, tag="bank")
         nc.tensor.matmul(out=bank_l[:, 0:256], lhsT=sel2[:], rhs=raw[:, 512:768], start=True, stop=True)
         nc.vector.tensor_scalar(
             out=lrow[:], in0=bank_l[:, 0:224], scalar1=1.0 / 3.0, scalar2=None, op0=MULT
         )
-        for s, (lm, rm, np_, r) in enumerate(terms):
-            cols = slice(r_off[s], r_off[s] + 4 * r)
-            nc.vector.tensor_copy(
-                out=rrow[:, cols].rearrange("p (d t) -> p d t", t=4),
-                in_=bank_r[:, cols].rearrange("p (t d) -> p d t", t=4),
-            )
+        nc.vector.tensor_copy(
+            out=rrow1[:].rearrange("p (d t) -> p d t", t=4),
+            in_=bank_r[:, 0:256].rearrange("p (t d) -> p d t", t=4),
+        )
         for h in range(2):
             bank_b = psum.tile([P, 512], F32, tag="bank")
             nc.tensor.matmul(
@@ -105,11 +109,18 @@ def tile_klinear_t_kernel(tc, x, L0, R0, L1, R1, L2, R2, bias, out):
             )
             nc.scalar.copy(out=bias_sb[:, 512 * h : 512 * h + 512], in_=bank_b[:])
 
-        for m in range(N_MACRO):
+        x_raw = {}
+
+        def x_load(m):
             xr = xpool.tile([P, 2048], BF16, tag="xr")
             nc.sync.dma_start(out=xr[:], in_=xv[m])
-            xw = xr[:].bitcast(F32)
-            xgw = xg[:, m, :].bitcast(F32)
+            x_raw[m] = xr
+
+        def x_prep(m):
+            if m not in x_raw:
+                x_load(m)
+            xw = x_raw[m][:].bitcast(F32)
+            xgw = xg[:, 2048 * m : 2048 * m + 2048].bitcast(F32)
             for j in range(2):
                 xt = psum.tile([P, 4, P], F32, tag="bank")
                 for g in range(2):
@@ -123,63 +134,118 @@ def tile_klinear_t_kernel(tc, x, L0, R0, L1, R1, L2, R2, bias, out):
                     in_=xt[:].rearrange("p (g u) m -> p g m u", u=2),
                 )
 
-        def w_term(s, g):
+        def w_term(s, h, g, part=None):
             lm, rm, np_, r = terms[s]
             w = 4 * r
-            rr = rrow[:, r_off[s] : r_off[s] + w]
-            for b in range(np_):
+            bs = list(range(h * np_ // 2, (h + 1) * np_ // 2))
+            if part is not None:
+                bs = bs[part]
+            for b in bs:
                 sc = lrow[:, l_off[s] + g * np_ + b : l_off[s] + g * np_ + b + 1]
                 dst = acc[:, g, w * b : w * b + w]
                 if s == 0:
-                    nc.vector.tensor_scalar(out=dst, in0=rr, scalar1=sc, scalar2=None, op0=MULT)
-                elif s == 1:
-                    nc.vector.scalar_tensor_tensor(out=dst, in0=rr, scalar=sc, in1=dst, op0=MULT, op1=ADD)
+                    if (h, g) in G_T1:
+                        nc.gpsimd.tensor_scalar(
+                            out=dst, in0=rrow1[:], scalar1=sc, scalar2=0.0, op0=MULT, op1=ADD
+                        )
+                    else:
+                        nc.vector.tensor_scalar(out=dst, in0=rrow1[:], scalar1=sc, scalar2=None, op0=MULT)
                 else:
+                    rr = bank_r[:, r_off[s] : r_off[s] + w].rearrange("p (t d) -> p d t", t=4)
+                    res = dst if s == 1 else wbf[:, g, w * b : w * b + w]
                     nc.vector.scalar_tensor_tensor(
-                        out=wbf[:, g, w * b : w * b + w], in0=rr, scalar=sc, in1=dst, op0=MULT, op1=ADD
+                        out=res.rearrange("p (d t) -> p d t", t=4),
+                        in0=rr,
+                        scalar=sc,
+                        in1=dst.rearrange("p (d t) -> p d t", t=4),
+                        op0=MULT,
+                        op1=ADD,
                     )
 
-        def w_quant(g):
-            nc.vector.quantize_mx(out=wc[:, g, :].bitcast(FP8X4), scales=ws[:, g, :], in_=wbf[:, g, :])
+        def w_quant(h, g):
+            nc.vector.quantize_mx(
+                out=wc[:, g, 512 * h : 512 * h + 512].bitcast(FP8X4),
+                scales=ws[:, g, 512 * h : 512 * h + 512],
+                in_=wbf[:, g, 2048 * h : 2048 * h + 2048],
+            )
 
-        def x_quant(m):
-            nc.vector.quantize_mx(out=xc[:, m, :].bitcast(FP8X4), scales=xs[:, m, :], in_=xg[:, m, :])
+        def x_quant(c):
+            nc.vector.quantize_mx(
+                out=xc[:, 1024 * c : 1024 * c + 1024].bitcast(FP8X4),
+                scales=xs[:, 1024 * c : 1024 * c + 1024],
+                in_=xg[:, 4096 * c : 4096 * c + 4096],
+            )
 
-        w_term(0, 0)
-        w_term(1, 0)
-        w_term(2, 0)
-        w_term(0, 1)
-        w_quant(0)
-        w_term(1, 1)
-        w_term(2, 1)
-        x_quant(0)
-        w_quant(1)
-        x_quant(1)
+        def product(m, j, h):
+            pb = psum.tile([P, 512], F32, tag="bank")
+            for g in range(2):
+                lo = 512 * m + 256 * j + 128 * g
+                nc.tensor.matmul_mx(
+                    out=pb[:],
+                    lhsT=xc[:, lo : lo + 128].bitcast(FP8X4),
+                    lhsT_scale=xs[:, lo : lo + 128],
+                    rhs=wc[:, g, 512 * h : 512 * h + 512].bitcast(FP8X4),
+                    rhs_scale=ws[:, g, 512 * h : 512 * h + 512],
+                    start=(g == 0),
+                    stop=(g == 1),
+                )
+            return pb
 
-        for m in range(N_MACRO):
-            ot = opool.tile([P, 2 * D], F32, tag="ot")
-            n_sg = 1 + (m % 2)
+        def leave(pb, dst, h, by_scalar):
+            bs = bias_sb[:, 512 * h : 512 * h + 512]
+            if by_scalar:
+                nc.scalar.copy(out=dst, in_=pb[:])
+                nc.gpsimd.tensor_tensor(out=dst, in0=dst, in1=bs, op=ADD)
+            else:
+                nc.vector.tensor_tensor(out=dst, in0=pb[:], in1=bs, op=ADD)
+
+        def half_macro(m, h, by_scalar):
+            oh = hpool.tile([P, 2, 512], F32, tag="oh")
             for j in range(2):
-                for h in range(2):
-                    pb = psum.tile([P, 512], F32, tag="bank")
-                    for g in range(2):
-                        cols = slice(256 * j + 128 * g, 256 * j + 128 * g + 128)
-                        nc.tensor.matmul_mx(
-                            out=pb[:],
-                            lhsT=xc[:, m, cols].bitcast(FP8X4),
-                            lhsT_scale=xs[:, m, cols],
-                            rhs=wc[:, g, 512 * h : 512 * h + 512].bitcast(FP8X4),
-                            rhs_scale=ws[:, g, 512 * h : 512 * h + 512],
-                            start=(g == 0),
-                            stop=(g == 1),
-                        )
-                    dst = ot[:, D * j + 512 * h : D * j + 512 * h + 512]
-                    bs = bias_sb[:, 512 * h : 512 * h + 512]
-                    if 2 * j + h >= 4 - n_sg:
-                        nc.scalar.copy(out=dst, in_=pb[:])
-                        nc.gpsimd.tensor_tensor(out=dst, in0=dst, in1=bs, op=ADD)
-                    else:
-                        nc.vector.tensor_tensor(out=dst, in0=pb[:], in1=bs, op=ADD)
-            if m + 2 < N_MACRO:
-                x_quant(m + 2)
+                leave(product(m, j, h), oh[:, j, :], h, by_scalar)
+            nc.sync.dma_start(out=ov3[m][:, :, 512 * h : 512 * h + 512], in_=oh[:])
+
+        for m in range(PRE_T):
+            x_prep(m)
+
+        for hg in [(0, 0), (0, 1), (1, 0), (1, 1)]:
+            w_term(0, hg[0], hg[1])
+        w_term(1, 0, 0)
+        w_term(2, 0, 0)
+        w_term(1, 0, 1)
+        w_term(2, 0, 1)
+        w_quant(0, 0)
+        w_term(1, 1, 0, slice(0, 4))
+        w_quant(0, 1)
+        for c in range((EARLY + 1) // 2):
+            x_quant(c)
+        for m in range(PRE_T, N_MACRO):
+            x_load(m)
+        for e in range(EARLY):
+            half_macro(e, 0, True)
+            if PRE_T + e < N_MACRO:
+                x_prep(PRE_T + e)
+        for m in range(PRE_T + EARLY, N_MACRO):
+            x_prep(m)
+        w_term(1, 1, 0, slice(4, 16))
+        w_term(2, 1, 0)
+        w_term(1, 1, 1)
+        w_quant(1, 0)
+        w_term(2, 1, 1)
+        for c in BURSTS.get(-2, []):
+            x_quant(c)
+        w_quant(1, 1)
+        for c in BURSTS.get(-1, []):
+            x_quant(c)
+
+        for m in range(EARLY):
+            half_macro(m, 1, False)
+        for m in range(EARLY, N_MACRO):
+            ot = opool.tile([P, 2 * D], F32, tag="ot")
+            n_sg = LATE_SG[m - EARLY]
+            for i in range(4):
+                j, h = divmod(i, 2)
+                leave(product(m, j, h), ot[:, D * j + 512 * h : D * j + 512 * h + 512], h, i < n_sg)
+            for c in BURSTS.get(m, []):
+                x_quant(c)
             nc.sync.dma_start(out=ov[m], in_=ot[:])

@@ -16,11 +16,169 @@ D = 1024
 TOKENS = 4096
 FLOPS = 2 * TOKENS * D * D
 N_MACRO = 16
-EARLY = 6
-PRE_T = 12
-LATE_SG = [1, 2, 1, 2, 1, 2, 1, 2, 1, 1]
-BURSTS = {-2: [3], -1: [4], 6: [5, 6], 10: [7]}
-G_T1 = [(0, 1), (1, 0), (1, 1)]
+STEPS = [
+    ("XL", 0),
+    ("XT", 0),
+    ("XL", 1),
+    ("XT", 1),
+    ("XL", 2),
+    ("XT", 2),
+    ("XL", 3),
+    ("XT", 3),
+    ("XL", 4),
+    ("XT", 4),
+    ("XL", 5),
+    ("XT", 5),
+    ("XL", 6),
+    ("XT", 6),
+    ("XL", 7),
+    ("XT", 7),
+    ("XL", 8),
+    ("XT", 8),
+    ("XL", 9),
+    ("XT", 9),
+    ("XL", 10),
+    ("XT", 10),
+    ("XL", 11),
+    ("XT", 11),
+    ("W", 0, 0, 0, 8, False),
+    ("W", 0, 1, 0, 8, True),
+    ("W", 0, 0, 8, 16, True),
+    ("W", 0, 1, 8, 16, True),
+    ("W", 1, 0, 0, 16, False),
+    ("W", 2, 0, 0, 32, False),
+    ("W", 1, 1, 0, 16, False),
+    ("W", 2, 1, 0, 32, False),
+    ("WQ", 0, 0),
+    ("W", 1, 0, 16, 20, False),
+    ("WQ", 0, 1),
+    ("XQ", 0),
+    ("XQ", 1),
+    ("XL", 12),
+    ("XL", 13),
+    ("XL", 14),
+    ("XL", 15),
+    ("OH", 0, 0),
+    ("B", 0, 0, 0, True),
+    ("B", 0, 1, 0, True),
+    ("SH", 0, 0),
+    ("XT", 12),
+    ("OH", 1, 0),
+    ("B", 1, 0, 0, True),
+    ("B", 1, 1, 0, True),
+    ("SH", 1, 0),
+    ("XT", 13),
+    ("OH", 2, 0),
+    ("B", 2, 0, 0, True),
+    ("B", 2, 1, 0, True),
+    ("SH", 2, 0),
+    ("XT", 14),
+    ("OH", 3, 0),
+    ("B", 3, 0, 0, True),
+    ("B", 3, 1, 0, True),
+    ("SH", 3, 0),
+    ("XT", 15),
+    ("W", 1, 0, 20, 32, False),
+    ("W", 2, 0, 32, 64, False),
+    ("W", 1, 1, 16, 32, False),
+    ("WQ", 1, 0),
+    ("W", 2, 1, 32, 64, False),
+    ("WQ", 1, 1),
+    ("XQ", 2),
+    ("OT2", 0, 1),
+    ("B", 0, 0, 1, False),
+    ("B", 0, 1, 1, False),
+    ("SH", 0, 1),
+    ("OT2", 1, 1),
+    ("B", 1, 0, 1, False),
+    ("B", 1, 1, 1, False),
+    ("SH", 1, 1),
+    ("XQ", 3),
+    ("XQ", 4),
+    ("OT2", 2, 1),
+    ("B", 2, 0, 1, False),
+    ("B", 2, 1, 1, False),
+    ("SH", 2, 1),
+    ("OH", 3, 1),
+    ("B", 3, 0, 1, True),
+    ("B", 3, 1, 1, True),
+    ("SH", 3, 1),
+    ("OT", 4),
+    ("B", 4, 0, 0, False),
+    ("B", 4, 0, 1, False),
+    ("B", 4, 1, 0, False),
+    ("B", 4, 1, 1, False),
+    ("SF", 4),
+    ("OT", 5),
+    ("B", 5, 0, 0, True),
+    ("B", 5, 1, 1, True),
+    ("B", 5, 0, 1, False),
+    ("B", 5, 1, 0, False),
+    ("SF", 5),
+    ("XQ", 5),
+    ("OT", 6),
+    ("B", 6, 1, 0, True),
+    ("B", 6, 0, 0, False),
+    ("B", 6, 0, 1, False),
+    ("B", 6, 1, 1, False),
+    ("SF", 6),
+    ("OT", 7),
+    ("B", 7, 0, 1, True),
+    ("B", 7, 0, 0, False),
+    ("B", 7, 1, 0, False),
+    ("B", 7, 1, 1, False),
+    ("SF", 7),
+    ("XQ", 6),
+    ("OT", 8),
+    ("B", 8, 1, 1, True),
+    ("B", 8, 0, 0, False),
+    ("B", 8, 0, 1, False),
+    ("B", 8, 1, 0, False),
+    ("SF", 8),
+    ("OT", 9),
+    ("B", 9, 1, 0, True),
+    ("B", 9, 0, 0, False),
+    ("B", 9, 0, 1, False),
+    ("B", 9, 1, 1, False),
+    ("SF", 9),
+    ("OT", 10),
+    ("B", 10, 0, 1, True),
+    ("B", 10, 0, 0, False),
+    ("B", 10, 1, 0, False),
+    ("B", 10, 1, 1, False),
+    ("SF", 10),
+    ("XQ", 7),
+    ("OT", 11),
+    ("B", 11, 1, 1, True),
+    ("B", 11, 0, 0, False),
+    ("B", 11, 0, 1, False),
+    ("B", 11, 1, 0, False),
+    ("SF", 11),
+    ("OT", 12),
+    ("B", 12, 1, 0, True),
+    ("B", 12, 0, 0, False),
+    ("B", 12, 0, 1, False),
+    ("B", 12, 1, 1, False),
+    ("SF", 12),
+    ("OT", 13),
+    ("B", 13, 0, 1, True),
+    ("B", 13, 0, 0, False),
+    ("B", 13, 1, 0, False),
+    ("B", 13, 1, 1, False),
+    ("SF", 13),
+    ("OT", 14),
+    ("B", 14, 1, 1, True),
+    ("B", 14, 0, 0, False),
+    ("B", 14, 0, 1, False),
+    ("B", 14, 1, 0, False),
+    ("SF", 14),
+    ("OT", 15),
+    ("B", 15, 1, 0, True),
+    ("B", 15, 0, 0, False),
+    ("B", 15, 0, 1, False),
+    ("B", 15, 1, 1, False),
+    ("SF", 15),
+]
 
 
 def tile_klinear_t_kernel(tc, x, L0, R0, L1, R1, L2, R2, bias, out):
@@ -134,17 +292,14 @@ def tile_klinear_t_kernel(tc, x, L0, R0, L1, R1, L2, R2, bias, out):
                     in_=xt[:].rearrange("p (g u) m -> p g m u", u=2),
                 )
 
-        def w_term(s, h, g, part=None):
+        def w_term(s, g, lo, hi, on_gpsimd):
             lm, rm, np_, r = terms[s]
             w = 4 * r
-            bs = list(range(h * np_ // 2, (h + 1) * np_ // 2))
-            if part is not None:
-                bs = bs[part]
-            for b in bs:
+            for b in range(lo, hi):
                 sc = lrow[:, l_off[s] + g * np_ + b : l_off[s] + g * np_ + b + 1]
                 dst = acc[:, g, w * b : w * b + w]
                 if s == 0:
-                    if (h, g) in G_T1:
+                    if on_gpsimd:
                         nc.gpsimd.tensor_scalar(
                             out=dst, in0=rrow1[:], scalar1=sc, scalar2=0.0, op0=MULT, op1=ADD
                         )
@@ -199,53 +354,38 @@ def tile_klinear_t_kernel(tc, x, L0, R0, L1, R1, L2, R2, bias, out):
             else:
                 nc.vector.tensor_tensor(out=dst, in0=pb[:], in1=bs, op=ADD)
 
-        def half_macro(m, h, by_scalar):
-            oh = hpool.tile([P, 2, 512], F32, tag="oh")
-            for j in range(2):
-                leave(product(m, j, h), oh[:, j, :], h, by_scalar)
-            nc.sync.dma_start(out=ov3[m][:, :, 512 * h : 512 * h + 512], in_=oh[:])
-
-        for m in range(PRE_T):
-            x_prep(m)
-
-        for hg in [(0, 0), (0, 1), (1, 0), (1, 1)]:
-            w_term(0, hg[0], hg[1])
-        w_term(1, 0, 0)
-        w_term(2, 0, 0)
-        w_term(1, 0, 1)
-        w_term(2, 0, 1)
-        w_quant(0, 0)
-        w_term(1, 1, 0, slice(0, 4))
-        w_quant(0, 1)
-        for c in range((EARLY + 1) // 2):
-            x_quant(c)
-        for m in range(PRE_T, N_MACRO):
-            x_load(m)
-        for e in range(EARLY):
-            half_macro(e, 0, True)
-            if PRE_T + e < N_MACRO:
-                x_prep(PRE_T + e)
-        for m in range(PRE_T + EARLY, N_MACRO):
-            x_prep(m)
-        w_term(1, 1, 0, slice(4, 16))
-        w_term(2, 1, 0)
-        w_term(1, 1, 1)
-        w_quant(1, 0)
-        w_term(2, 1, 1)
-        for c in BURSTS.get(-2, []):
-            x_quant(c)
-        w_quant(1, 1)
-        for c in BURSTS.get(-1, []):
-            x_quant(c)
-
-        for m in range(EARLY):
-            half_macro(m, 1, False)
-        for m in range(EARLY, N_MACRO):
-            ot = opool.tile([P, 2 * D], F32, tag="ot")
-            n_sg = LATE_SG[m - EARLY]
-            for i in range(4):
-                j, h = divmod(i, 2)
-                leave(product(m, j, h), ot[:, D * j + 512 * h : D * j + 512 * h + 512], h, i < n_sg)
-            for c in BURSTS.get(m, []):
-                x_quant(c)
-            nc.sync.dma_start(out=ov[m], in_=ot[:])
+        o_tiles = {}
+        for step in STEPS:
+            kind = step[0]
+            if kind == "XL":
+                x_load(step[1])
+            elif kind == "XT":
+                x_prep(step[1])
+            elif kind == "W":
+                w_term(step[1], step[2], step[3], step[4], step[5])
+            elif kind == "WQ":
+                w_quant(step[1], step[2])
+            elif kind == "XQ":
+                x_quant(step[1])
+            elif kind == "OH":
+                o_tiles[(step[1], step[2])] = hpool.tile([P, 2, 512], F32, tag="oh", name="oh")
+            elif kind == "OT2":
+                o_tiles[(step[1], step[2])] = opool.tile([P, 2, 512], F32, tag="ot", name="ot")
+            elif kind == "OT":
+                o_tiles[step[1]] = opool.tile([P, 2, D], F32, tag="ot", name="ot")
+            elif kind == "B":
+                m, j, h = step[1], step[2], step[3]
+                if (m, h) in o_tiles:
+                    dst = o_tiles[(m, h)][:, j, :]
+                else:
+                    dst = o_tiles[m][:, j, 512 * h : 512 * h + 512]
+                leave(product(m, j, h), dst, h, step[4])
+            elif kind == "SH":
+                m, h = step[1], step[2]
+                nc.sync.dma_start(out=ov3[m][:, :, 512 * h : 512 * h + 512], in_=o_tiles[(m, h)][:])
+            elif kind == "SJ":
+                m, j = step[1], step[2]
+                nc.sync.dma_start(out=ov3[m][:, j, :], in_=o_tiles[m][:, j, :])
+            else:
+                assert kind == "SF"
+                nc.sync.dma_start(out=ov3[step[1]], in_=o_tiles[step[1]][:])

@@ -13,172 +13,13 @@ ADD = mybir.AluOpType.add
 
 P = 128
 D = 1024
+HALF = 512
 TOKENS = 4096
 FLOPS = 2 * TOKENS * D * D
 N_MACRO = 16
-STEPS = [
-    ("XL", 0),
-    ("XT", 0),
-    ("XL", 1),
-    ("XT", 1),
-    ("XL", 2),
-    ("XT", 2),
-    ("XL", 3),
-    ("XT", 3),
-    ("XL", 4),
-    ("XT", 4),
-    ("XL", 5),
-    ("XT", 5),
-    ("XL", 6),
-    ("XT", 6),
-    ("XL", 7),
-    ("XT", 7),
-    ("XL", 8),
-    ("XT", 8),
-    ("XL", 9),
-    ("XT", 9),
-    ("XL", 10),
-    ("XT", 10),
-    ("XL", 11),
-    ("XT", 11),
-    ("W", 0, 0, 0, 8, False),
-    ("W", 0, 1, 0, 8, True),
-    ("W", 0, 0, 8, 16, True),
-    ("W", 0, 1, 8, 16, True),
-    ("W", 1, 0, 0, 16, False),
-    ("W", 2, 0, 0, 32, False),
-    ("W", 1, 1, 0, 16, False),
-    ("W", 2, 1, 0, 32, False),
-    ("WQ", 0, 0),
-    ("W", 1, 0, 16, 20, False),
-    ("WQ", 0, 1),
-    ("XQ", 0),
-    ("XQ", 1),
-    ("XL", 12),
-    ("XL", 13),
-    ("XL", 14),
-    ("XL", 15),
-    ("OH", 0, 0),
-    ("B", 0, 0, 0, True),
-    ("B", 0, 1, 0, True),
-    ("SH", 0, 0),
-    ("XT", 12),
-    ("OH", 1, 0),
-    ("B", 1, 0, 0, True),
-    ("B", 1, 1, 0, True),
-    ("SH", 1, 0),
-    ("XT", 13),
-    ("OH", 2, 0),
-    ("B", 2, 0, 0, True),
-    ("B", 2, 1, 0, True),
-    ("SH", 2, 0),
-    ("XT", 14),
-    ("OH", 3, 0),
-    ("B", 3, 0, 0, True),
-    ("B", 3, 1, 0, True),
-    ("SH", 3, 0),
-    ("XT", 15),
-    ("W", 1, 0, 20, 32, False),
-    ("W", 2, 0, 32, 64, False),
-    ("W", 1, 1, 16, 32, False),
-    ("WQ", 1, 0),
-    ("W", 2, 1, 32, 64, False),
-    ("WQ", 1, 1),
-    ("XQ", 2),
-    ("OT2", 0, 1),
-    ("B", 0, 0, 1, False),
-    ("B", 0, 1, 1, False),
-    ("SH", 0, 1),
-    ("OT2", 1, 1),
-    ("B", 1, 0, 1, False),
-    ("B", 1, 1, 1, False),
-    ("SH", 1, 1),
-    ("XQ", 3),
-    ("XQ", 4),
-    ("OT2", 2, 1),
-    ("B", 2, 0, 1, False),
-    ("B", 2, 1, 1, False),
-    ("SH", 2, 1),
-    ("OH", 3, 1),
-    ("B", 3, 0, 1, True),
-    ("B", 3, 1, 1, True),
-    ("SH", 3, 1),
-    ("OT", 4),
-    ("B", 4, 0, 0, False),
-    ("B", 4, 0, 1, False),
-    ("B", 4, 1, 0, False),
-    ("B", 4, 1, 1, False),
-    ("SF", 4),
-    ("OT", 5),
-    ("B", 5, 0, 0, True),
-    ("B", 5, 1, 1, True),
-    ("B", 5, 0, 1, False),
-    ("B", 5, 1, 0, False),
-    ("SF", 5),
-    ("XQ", 5),
-    ("OT", 6),
-    ("B", 6, 1, 0, True),
-    ("B", 6, 0, 0, False),
-    ("B", 6, 0, 1, False),
-    ("B", 6, 1, 1, False),
-    ("SF", 6),
-    ("OT", 7),
-    ("B", 7, 0, 1, True),
-    ("B", 7, 0, 0, False),
-    ("B", 7, 1, 0, False),
-    ("B", 7, 1, 1, False),
-    ("SF", 7),
-    ("XQ", 6),
-    ("OT", 8),
-    ("B", 8, 1, 1, True),
-    ("B", 8, 0, 0, False),
-    ("B", 8, 0, 1, False),
-    ("B", 8, 1, 0, False),
-    ("SF", 8),
-    ("OT", 9),
-    ("B", 9, 1, 0, True),
-    ("B", 9, 0, 0, False),
-    ("B", 9, 0, 1, False),
-    ("B", 9, 1, 1, False),
-    ("SF", 9),
-    ("OT", 10),
-    ("B", 10, 0, 1, True),
-    ("B", 10, 0, 0, False),
-    ("B", 10, 1, 0, False),
-    ("B", 10, 1, 1, False),
-    ("SF", 10),
-    ("XQ", 7),
-    ("OT", 11),
-    ("B", 11, 1, 1, True),
-    ("B", 11, 0, 0, False),
-    ("B", 11, 0, 1, False),
-    ("B", 11, 1, 0, False),
-    ("SF", 11),
-    ("OT", 12),
-    ("B", 12, 1, 0, True),
-    ("B", 12, 0, 0, False),
-    ("B", 12, 0, 1, False),
-    ("B", 12, 1, 1, False),
-    ("SF", 12),
-    ("OT", 13),
-    ("B", 13, 0, 1, True),
-    ("B", 13, 0, 0, False),
-    ("B", 13, 1, 0, False),
-    ("B", 13, 1, 1, False),
-    ("SF", 13),
-    ("OT", 14),
-    ("B", 14, 1, 1, True),
-    ("B", 14, 0, 0, False),
-    ("B", 14, 0, 1, False),
-    ("B", 14, 1, 0, False),
-    ("SF", 14),
-    ("OT", 15),
-    ("B", 15, 1, 0, True),
-    ("B", 15, 0, 0, False),
-    ("B", 15, 0, 1, False),
-    ("B", 15, 1, 1, False),
-    ("SF", 15),
-]
+EARLY = 5
+FIRST_T = 12
+QUANT_LEAD = 2
 
 
 def tile_klinear_t_kernel(tc, x, L0, R0, L1, R1, L2, R2, bias, out):
@@ -187,13 +28,11 @@ def tile_klinear_t_kernel(tc, x, L0, R0, L1, R1, L2, R2, bias, out):
     r_off = [0, 256, 384]
     l_off = [0, 32, 96]
     xv = x.flatten_outer_dims().rearrange("(m p j) k -> m p (j k)", p=P, j=2)
-    ov = out.flatten_outer_dims().rearrange("(m p j) n -> m p (j n)", p=P, j=2)
-    ov3 = out.flatten_outer_dims().rearrange("(m p j) n -> m p j n", p=P, j=2)
+    ov = out.flatten_outer_dims().rearrange("(m p j) n -> m p j n", p=P, j=2)
 
     with ExitStack() as ctx:
         keep = ctx.enter_context(tc.tile_pool(name="keep", bufs=1))
         xpool = ctx.enter_context(tc.tile_pool(name="xpool", bufs=4))
-        opool = ctx.enter_context(tc.tile_pool(name="opool", bufs=3))
         hpool = ctx.enter_context(tc.tile_pool(name="hpool", bufs=4))
         psum_r = ctx.enter_context(tc.psum_pool(name="psum_r", bufs=1))
         psum = ctx.enter_context(tc.psum_pool(name="psum", bufs=7))
@@ -207,13 +46,11 @@ def tile_klinear_t_kernel(tc, x, L0, R0, L1, R1, L2, R2, bias, out):
         rrow1 = keep.tile([P, 256], F32)
         lrow = keep.tile([P, 224], F32)
         bias_sb = keep.tile([P, D], F32)
-        acc = keep.tile([P, 2, 4 * D], F32)
-        wbf = keep.tile([P, 2, 4 * D], BF16, align_bytes=64)
         wc = keep.tile([P, 2, D], U32, align_bytes=64)
         ws = keep.tile([P, 2, D], U8, align_bytes=64)
         xg = keep.tile([P, N_MACRO * 2048], BF16, align_bytes=64)
-        xc = keep.tile([P, N_MACRO * 512], U32, align_bytes=64)
-        xs = keep.tile([P, N_MACRO * 512], U8, align_bytes=64)
+        xc = keep.tile([P, N_MACRO * HALF], U32, align_bytes=64)
+        xs = keep.tile([P, N_MACRO * HALF], U8, align_bytes=64)
 
         nc.vector.memset(raw[:].bitcast(F32), 0.0)
         make_identity(nc, ident[:])
@@ -224,9 +61,9 @@ def tile_klinear_t_kernel(tc, x, L0, R0, L1, R1, L2, R2, bias, out):
                 in_=rm.rearrange("(q t) d -> q (t d)", t=4),
             )
         for s, (lm, rm, np_, r) in enumerate(terms):
-            ns = 512 // r
+            ns = HALF // r
             nc.sync.dma_start(
-                out=raw[32 * s : 32 * s + ns, 512 + l_off[s] : 512 + l_off[s] + 2 * np_].rearrange(
+                out=raw[32 * s : 32 * s + ns, HALF + l_off[s] : HALF + l_off[s] + 2 * np_].rearrange(
                     "s (g b) -> s g b", g=2
                 ),
                 in_=lm.rearrange("(g s) b -> s g b", g=2),
@@ -236,7 +73,7 @@ def tile_klinear_t_kernel(tc, x, L0, R0, L1, R1, L2, R2, bias, out):
 
         for s, (lm, rm, np_, r) in enumerate(terms):
             nq = r // 4
-            ns = 512 // r
+            ns = HALF // r
             rows = slice(32 * s, 32 * s + 32)
             nc.vector.tensor_copy(
                 out=sel1[rows, :].rearrange("k (a b) -> k a b", b=nq),
@@ -249,10 +86,10 @@ def tile_klinear_t_kernel(tc, x, L0, R0, L1, R1, L2, R2, bias, out):
         nc.vector.tensor_copy(out=sel1[96:128, :], in_=ident[96:128, 96:97].to_broadcast([32, P]))
         nc.vector.memset(sel2[96:128, :], 0.0)
 
-        bank_r = psum_r.tile([P, 512], F32)
-        nc.tensor.matmul(out=bank_r[:], lhsT=sel1[:], rhs=raw[:, 0:512], start=True, stop=True)
-        bank_l = psum.tile([P, 512], F32, tag="bank")
-        nc.tensor.matmul(out=bank_l[:, 0:256], lhsT=sel2[:], rhs=raw[:, 512:768], start=True, stop=True)
+        bank_r = psum_r.tile([P, HALF], F32)
+        nc.tensor.matmul(out=bank_r[:], lhsT=sel1[:], rhs=raw[:, 0:HALF], start=True, stop=True)
+        bank_l = psum.tile([P, HALF], F32, tag="bank")
+        nc.tensor.matmul(out=bank_l[:, 0:256], lhsT=sel2[:], rhs=raw[:, HALF:768], start=True, stop=True)
         nc.vector.tensor_scalar(
             out=lrow[:], in0=bank_l[:, 0:224], scalar1=1.0 / 3.0, scalar2=None, op0=MULT
         )
@@ -261,11 +98,11 @@ def tile_klinear_t_kernel(tc, x, L0, R0, L1, R1, L2, R2, bias, out):
             in_=bank_r[:, 0:256].rearrange("p (t d) -> p d t", t=4),
         )
         for h in range(2):
-            bank_b = psum.tile([P, 512], F32, tag="bank")
+            bank_b = psum.tile([P, HALF], F32, tag="bank")
             nc.tensor.matmul(
-                out=bank_b[:], lhsT=sel1[:], rhs=rawb[:, 512 * h : 512 * h + 512], start=True, stop=True
+                out=bank_b[:], lhsT=sel1[:], rhs=rawb[:, HALF * h : HALF * h + HALF], start=True, stop=True
             )
-            nc.scalar.copy(out=bias_sb[:, 512 * h : 512 * h + 512], in_=bank_b[:])
+            nc.scalar.copy(out=bias_sb[:, HALF * h : HALF * h + HALF], in_=bank_b[:])
 
         x_raw = {}
 
@@ -274,55 +111,21 @@ def tile_klinear_t_kernel(tc, x, L0, R0, L1, R1, L2, R2, bias, out):
             nc.sync.dma_start(out=xr[:], in_=xv[m])
             x_raw[m] = xr
 
-        def x_prep(m):
-            if m not in x_raw:
-                x_load(m)
+        def x_transpose(m):
             xw = x_raw[m][:].bitcast(F32)
             xgw = xg[:, 2048 * m : 2048 * m + 2048].bitcast(F32)
             for j in range(2):
                 xt = psum.tile([P, 4, P], F32, tag="bank")
                 for g in range(2):
-                    words = xw[:, 512 * j + 256 * g : 512 * j + 256 * g + 256].rearrange(
+                    words = xw[:, HALF * j + 256 * g : HALF * j + 256 * g + 256].rearrange(
                         "m (p u) -> m u p", u=2
                     )
                     for u in range(2):
                         nc.tensor.transpose(xt[:, 2 * g + u, :], words[:, u, :], ident[:])
                 nc.scalar.copy(
-                    out=xgw[:, 512 * j : 512 * j + 512].rearrange("p (g m u) -> p g m u", g=2, u=2),
+                    out=xgw[:, HALF * j : HALF * j + HALF].rearrange("p (g m u) -> p g m u", g=2, u=2),
                     in_=xt[:].rearrange("p (g u) m -> p g m u", u=2),
                 )
-
-        def w_term(s, g, lo, hi, on_gpsimd):
-            lm, rm, np_, r = terms[s]
-            w = 4 * r
-            for b in range(lo, hi):
-                sc = lrow[:, l_off[s] + g * np_ + b : l_off[s] + g * np_ + b + 1]
-                dst = acc[:, g, w * b : w * b + w]
-                if s == 0:
-                    if on_gpsimd:
-                        nc.gpsimd.tensor_scalar(
-                            out=dst, in0=rrow1[:], scalar1=sc, scalar2=0.0, op0=MULT, op1=ADD
-                        )
-                    else:
-                        nc.vector.tensor_scalar(out=dst, in0=rrow1[:], scalar1=sc, scalar2=None, op0=MULT)
-                else:
-                    rr = bank_r[:, r_off[s] : r_off[s] + w].rearrange("p (t d) -> p d t", t=4)
-                    res = dst if s == 1 else wbf[:, g, w * b : w * b + w]
-                    nc.vector.scalar_tensor_tensor(
-                        out=res.rearrange("p (d t) -> p d t", t=4),
-                        in0=rr,
-                        scalar=sc,
-                        in1=dst.rearrange("p (d t) -> p d t", t=4),
-                        op0=MULT,
-                        op1=ADD,
-                    )
-
-        def w_quant(h, g):
-            nc.vector.quantize_mx(
-                out=wc[:, g, 512 * h : 512 * h + 512].bitcast(FP8X4),
-                scales=ws[:, g, 512 * h : 512 * h + 512],
-                in_=wbf[:, g, 2048 * h : 2048 * h + 2048],
-            )
 
         def x_quant(c):
             nc.vector.quantize_mx(
@@ -332,60 +135,112 @@ def tile_klinear_t_kernel(tc, x, L0, R0, L1, R1, L2, R2, bias, out):
             )
 
         def product(m, j, h):
-            pb = psum.tile([P, 512], F32, tag="bank")
+            pb = psum.tile([P, HALF], F32, tag="bank")
             for g in range(2):
-                lo = 512 * m + 256 * j + 128 * g
+                lo = HALF * m + 256 * j + P * g
                 nc.tensor.matmul_mx(
                     out=pb[:],
-                    lhsT=xc[:, lo : lo + 128].bitcast(FP8X4),
-                    lhsT_scale=xs[:, lo : lo + 128],
-                    rhs=wc[:, g, 512 * h : 512 * h + 512].bitcast(FP8X4),
-                    rhs_scale=ws[:, g, 512 * h : 512 * h + 512],
+                    lhsT=xc[:, lo : lo + P].bitcast(FP8X4),
+                    lhsT_scale=xs[:, lo : lo + P],
+                    rhs=wc[:, g, HALF * h : HALF * h + HALF].bitcast(FP8X4),
+                    rhs_scale=ws[:, g, HALF * h : HALF * h + HALF],
                     start=(g == 0),
                     stop=(g == 1),
                 )
             return pb
 
         def leave(pb, dst, h, by_scalar):
-            bs = bias_sb[:, 512 * h : 512 * h + 512]
+            bs = bias_sb[:, HALF * h : HALF * h + HALF]
             if by_scalar:
                 nc.scalar.copy(out=dst, in_=pb[:])
                 nc.gpsimd.tensor_tensor(out=dst, in0=dst, in1=bs, op=ADD)
             else:
                 nc.vector.tensor_tensor(out=dst, in0=pb[:], in1=bs, op=ADD)
 
-        o_tiles = {}
-        for step in STEPS:
-            kind = step[0]
-            if kind == "XL":
-                x_load(step[1])
-            elif kind == "XT":
-                x_prep(step[1])
-            elif kind == "W":
-                w_term(step[1], step[2], step[3], step[4], step[5])
-            elif kind == "WQ":
-                w_quant(step[1], step[2])
-            elif kind == "XQ":
-                x_quant(step[1])
-            elif kind == "OH":
-                o_tiles[(step[1], step[2])] = hpool.tile([P, 2, 512], F32, tag="oh", name="oh")
-            elif kind == "OT2":
-                o_tiles[(step[1], step[2])] = opool.tile([P, 2, 512], F32, tag="ot", name="ot")
-            elif kind == "OT":
-                o_tiles[step[1]] = opool.tile([P, 2, D], F32, tag="ot", name="ot")
-            elif kind == "B":
-                m, j, h = step[1], step[2], step[3]
-                if (m, h) in o_tiles:
-                    dst = o_tiles[(m, h)][:, j, :]
-                else:
-                    dst = o_tiles[m][:, j, 512 * h : 512 * h + 512]
-                leave(product(m, j, h), dst, h, step[4])
-            elif kind == "SH":
-                m, h = step[1], step[2]
-                nc.sync.dma_start(out=ov3[m][:, :, 512 * h : 512 * h + 512], in_=o_tiles[(m, h)][:])
-            elif kind == "SJ":
-                m, j = step[1], step[2]
-                nc.sync.dma_start(out=ov3[m][:, j, :], in_=o_tiles[m][:, j, :])
-            else:
-                assert kind == "SF"
-                nc.sync.dma_start(out=ov3[step[1]], in_=o_tiles[step[1]][:])
+        def half_rows(pool, tag, m, h, n_scalar):
+            oh = pool.tile([P, 2, HALF], F32, tag=tag, name=tag)
+            for j in range(2):
+                leave(product(m, j, h), oh[:, j, :], h, j < n_scalar)
+            nc.sync.dma_start(out=ov[m][:, :, HALF * h : HALF * h + HALF], in_=oh[:])
+
+        for m in range(FIRST_T):
+            x_load(m)
+            x_transpose(m)
+
+        with tc.tile_pool(name="wpool", bufs=1) as wpool:
+            acc = wpool.tile([P, 2, 4 * D], F32)
+            wbf = wpool.tile([P, 2, 4 * D], BF16, align_bytes=64)
+
+            def w_term(s, h, g, first=0, last=None, on_gpsimd=False):
+                lm, rm, np_, r = terms[s]
+                w = 4 * r
+                for b in list(range(h * np_ // 2, (h + 1) * np_ // 2))[first:last]:
+                    sc = lrow[:, l_off[s] + g * np_ + b : l_off[s] + g * np_ + b + 1]
+                    dst = acc[:, g, w * b : w * b + w]
+                    if s == 0 and on_gpsimd:
+                        nc.gpsimd.tensor_scalar(
+                            out=dst, in0=rrow1[:], scalar1=sc, scalar2=0.0, op0=MULT, op1=ADD
+                        )
+                    elif s == 0:
+                        nc.vector.tensor_scalar(out=dst, in0=rrow1[:], scalar1=sc, scalar2=None, op0=MULT)
+                    else:
+                        res = dst if s == 1 else wbf[:, g, w * b : w * b + w]
+                        nc.vector.scalar_tensor_tensor(
+                            out=res.rearrange("p (d t) -> p d t", t=4),
+                            in0=bank_r[:, r_off[s] : r_off[s] + w].rearrange("p (t d) -> p d t", t=4),
+                            scalar=sc,
+                            in1=dst.rearrange("p (d t) -> p d t", t=4),
+                            op0=MULT,
+                            op1=ADD,
+                        )
+
+            def w_quant(h, g):
+                nc.vector.quantize_mx(
+                    out=wc[:, g, HALF * h : HALF * h + HALF].bitcast(FP8X4),
+                    scales=ws[:, g, HALF * h : HALF * h + HALF],
+                    in_=wbf[:, g, 2048 * h : 2048 * h + 2048],
+                )
+
+            w_term(0, 0, 0)
+            w_term(0, 0, 1, on_gpsimd=True)
+            w_term(0, 1, 0, on_gpsimd=True)
+            w_term(0, 1, 1, on_gpsimd=True)
+            for g in range(2):
+                w_term(1, 0, g)
+                w_term(2, 0, g)
+            w_quant(0, 0)
+            w_term(1, 1, 0, last=4)
+            w_quant(0, 1)
+            for c in range((EARLY + 1) // 2):
+                x_quant(c)
+            for m in range(FIRST_T, N_MACRO):
+                x_load(m)
+            for e in range(EARLY):
+                half_rows(hpool, "oh", e, 0, 2)
+                if FIRST_T + e < N_MACRO:
+                    x_transpose(FIRST_T + e)
+            w_term(1, 1, 0, first=4)
+            w_term(2, 1, 0)
+            w_term(1, 1, 1)
+            w_quant(1, 0)
+            w_term(2, 1, 1)
+            w_quant(1, 1)
+
+        opool = ctx.enter_context(tc.tile_pool(name="opool", bufs=6))
+        for m in range(N_MACRO):
+            c = (m + QUANT_LEAD) // 2
+            if (m + QUANT_LEAD) % 2 == 0 and (EARLY + 1) // 2 <= c < N_MACRO // 2:
+                x_quant(c)
+            if m < EARLY:
+                half_rows(opool, "ot", m, 1, 1 - m % 2)
+                continue
+            last = m == N_MACRO - 1
+            ot = opool.tile([P, 2, D], F32, tag="ot")
+            for j in range(2):
+                for h in range(2):
+                    by_scalar = j == 0 and h == 0 and not last
+                    leave(product(m, j, h), ot[:, j, HALF * h : HALF * h + HALF], h, by_scalar)
+                if last:
+                    nc.sync.dma_start(out=ov[m][:, j, :], in_=ot[:, j, :])
+            if not last:
+                nc.sync.dma_start(out=ov[m], in_=ot[:])

@@ -46,8 +46,8 @@ def tile_klinear_t_kernel(tc, x, L0, R0, L1, R1, L2, R2, bias, out):
         rrow1 = keep.tile([P, 256], F32)
         lrow = keep.tile([P, 224], F32)
         bias_sb = keep.tile([P, D], F32)
-        wc = keep.tile([P, 2, D], U32, align_bytes=64)
-        ws = keep.tile([P, 2, D], U8, align_bytes=64)
+        wc = keep.tile([P, 4 * HALF], U32, align_bytes=64)
+        ws = keep.tile([P, 4 * HALF], U8, align_bytes=64)
         xg = keep.tile([P, N_MACRO * 2048], BF16, align_bytes=64)
         xc = keep.tile([P, N_MACRO * HALF], U32, align_bytes=64)
         xs = keep.tile([P, N_MACRO * HALF], U8, align_bytes=64)
@@ -56,12 +56,11 @@ def tile_klinear_t_kernel(tc, x, L0, R0, L1, R1, L2, R2, bias, out):
         make_identity(nc, ident[:])
         for s, (lm, rm, np_, r) in enumerate(terms):
             nq = r // 4
+            ns = HALF // r
             nc.sync.dma_start(
                 out=raw[32 * s : 32 * s + nq, r_off[s] : r_off[s] + 4 * r],
                 in_=rm.rearrange("(q t) d -> q (t d)", t=4),
             )
-        for s, (lm, rm, np_, r) in enumerate(terms):
-            ns = HALF // r
             nc.sync.dma_start(
                 out=raw[32 * s : 32 * s + ns, HALF + l_off[s] : HALF + l_off[s] + 2 * np_].rearrange(
                     "s (g b) -> s g b", g=2
@@ -87,16 +86,21 @@ def tile_klinear_t_kernel(tc, x, L0, R0, L1, R1, L2, R2, bias, out):
         nc.vector.memset(sel2[96:128, :], 0.0)
 
         bank_r = psum_r.tile([P, HALF], F32)
-        nc.tensor.matmul(out=bank_r[:], lhsT=sel1[:], rhs=raw[:, 0:HALF], start=True, stop=True)
-        bank_l = psum.tile([P, HALF], F32, tag="bank")
-        nc.tensor.matmul(out=bank_l[:, 0:256], lhsT=sel2[:], rhs=raw[:, HALF:768], start=True, stop=True)
-        nc.vector.tensor_scalar(
-            out=lrow[:], in0=bank_l[:, 0:224], scalar1=1.0 / 3.0, scalar2=None, op0=MULT
+        nc.tensor.matmul(out=bank_r[:, 0:256], lhsT=sel1[:], rhs=raw[:, 0:256], start=True, stop=True)
+        bank_l1 = psum.tile([P, HALF], F32, tag="bank")
+        nc.tensor.matmul(
+            out=bank_l1[:, 0:32], lhsT=sel2[:], rhs=raw[:, HALF : HALF + 32], start=True, stop=True
         )
         nc.vector.tensor_copy(
             out=rrow1[:].rearrange("p (d t) -> p d t", t=4),
             in_=bank_r[:, 0:256].rearrange("p (t d) -> p d t", t=4),
         )
+        nc.vector.tensor_scalar(
+            out=lrow[:, 0:32], in0=bank_l1[:, 0:32], scalar1=1.0 / 3.0, scalar2=None, op0=MULT
+        )
+        nc.tensor.matmul(out=bank_r[:, 256:HALF], lhsT=sel1[:], rhs=raw[:, 256:HALF], start=True, stop=True)
+        bank_l = psum.tile([P, HALF], F32, tag="bank")
+        nc.tensor.matmul(out=bank_l[:, 0:256], lhsT=sel2[:], rhs=raw[:, HALF:768], start=True, stop=True)
         for h in range(2):
             bank_b = psum.tile([P, HALF], F32, tag="bank")
             nc.tensor.matmul(
@@ -142,8 +146,8 @@ def tile_klinear_t_kernel(tc, x, L0, R0, L1, R1, L2, R2, bias, out):
                     out=pb[:],
                     lhsT=xc[:, lo : lo + P].bitcast(FP8X4),
                     lhsT_scale=xs[:, lo : lo + P],
-                    rhs=wc[:, g, HALF * h : HALF * h + HALF].bitcast(FP8X4),
-                    rhs_scale=ws[:, g, HALF * h : HALF * h + HALF],
+                    rhs=wc[:, HALF * (2 * h + g) : HALF * (2 * h + g) + HALF].bitcast(FP8X4),
+                    rhs_scale=ws[:, HALF * (2 * h + g) : HALF * (2 * h + g) + HALF],
                     start=(g == 0),
                     stop=(g == 1),
                 )
@@ -168,15 +172,17 @@ def tile_klinear_t_kernel(tc, x, L0, R0, L1, R1, L2, R2, bias, out):
             x_transpose(m)
 
         with tc.tile_pool(name="wpool", bufs=1) as wpool:
-            acc = wpool.tile([P, 2, 4 * D], F32)
-            wbf = wpool.tile([P, 2, 4 * D], BF16, align_bytes=64)
+            acc = wpool.tile([P, 8 * D], F32)
+            wbf = wpool.tile([P, 8 * D], BF16, align_bytes=64)
 
             def w_term(s, h, g, first=0, last=None, on_gpsimd=False):
                 lm, rm, np_, r = terms[s]
                 w = 4 * r
-                for b in list(range(h * np_ // 2, (h + 1) * np_ // 2))[first:last]:
+                for i in list(range(np_ // 2))[first:last]:
+                    b = h * np_ // 2 + i
                     sc = lrow[:, l_off[s] + g * np_ + b : l_off[s] + g * np_ + b + 1]
-                    dst = acc[:, g, w * b : w * b + w]
+                    lo = 2048 * (2 * h + g) + w * i
+                    dst = acc[:, lo : lo + w]
                     if s == 0 and on_gpsimd:
                         nc.gpsimd.tensor_scalar(
                             out=dst, in0=rrow1[:], scalar1=sc, scalar2=0.0, op0=MULT, op1=ADD
@@ -184,7 +190,7 @@ def tile_klinear_t_kernel(tc, x, L0, R0, L1, R1, L2, R2, bias, out):
                     elif s == 0:
                         nc.vector.tensor_scalar(out=dst, in0=rrow1[:], scalar1=sc, scalar2=None, op0=MULT)
                     else:
-                        res = dst if s == 1 else wbf[:, g, w * b : w * b + w]
+                        res = dst if s == 1 else wbf[:, lo : lo + w]
                         nc.vector.scalar_tensor_tensor(
                             out=res.rearrange("p (d t) -> p d t", t=4),
                             in0=bank_r[:, r_off[s] : r_off[s] + w].rearrange("p (t d) -> p d t", t=4),
@@ -194,23 +200,25 @@ def tile_klinear_t_kernel(tc, x, L0, R0, L1, R1, L2, R2, bias, out):
                             op1=ADD,
                         )
 
-            def w_quant(h, g):
+            def w_quant(h):
                 nc.vector.quantize_mx(
-                    out=wc[:, g, HALF * h : HALF * h + HALF].bitcast(FP8X4),
-                    scales=ws[:, g, HALF * h : HALF * h + HALF],
-                    in_=wbf[:, g, 2048 * h : 2048 * h + 2048],
+                    out=wc[:, D * h : D * h + D].bitcast(FP8X4),
+                    scales=ws[:, D * h : D * h + D],
+                    in_=wbf[:, 4 * D * h : 4 * D * h + 4 * D],
                 )
 
             w_term(0, 0, 0)
+            nc.vector.tensor_scalar(
+                out=lrow[:, 32:224], in0=bank_l[:, 32:224], scalar1=1.0 / 3.0, scalar2=None, op0=MULT
+            )
             w_term(0, 0, 1, on_gpsimd=True)
             w_term(0, 1, 0, on_gpsimd=True)
             w_term(0, 1, 1, on_gpsimd=True)
             for g in range(2):
                 w_term(1, 0, g)
                 w_term(2, 0, g)
-            w_quant(0, 0)
             w_term(1, 1, 0, last=4)
-            w_quant(0, 1)
+            w_quant(0)
             for c in range((EARLY + 1) // 2):
                 x_quant(c)
             for m in range(FIRST_T, N_MACRO):
@@ -222,9 +230,8 @@ def tile_klinear_t_kernel(tc, x, L0, R0, L1, R1, L2, R2, bias, out):
             w_term(1, 1, 0, first=4)
             w_term(2, 1, 0)
             w_term(1, 1, 1)
-            w_quant(1, 0)
             w_term(2, 1, 1)
-            w_quant(1, 1)
+            w_quant(1)
 
         opool = ctx.enter_context(tc.tile_pool(name="opool", bufs=6))
         for m in range(N_MACRO):
@@ -239,8 +246,9 @@ def tile_klinear_t_kernel(tc, x, L0, R0, L1, R1, L2, R2, bias, out):
             for j in range(2):
                 for h in range(2):
                     by_scalar = j == 0 and h == 0 and not last
-                    leave(product(m, j, h), ot[:, j, HALF * h : HALF * h + HALF], h, by_scalar)
-                if last:
-                    nc.sync.dma_start(out=ov[m][:, j, :], in_=ot[:, j, :])
+                    cols = slice(HALF * h, HALF * h + HALF)
+                    leave(product(m, j, h), ot[:, j, cols], h, by_scalar)
+                    if last:
+                        nc.sync.dma_start(out=ov[m][:, j, cols], in_=ot[:, j, cols])
             if not last:
                 nc.sync.dma_start(out=ov[m], in_=ot[:])

@@ -46,11 +46,11 @@ def tile_klinear_t_kernel(tc, x, L0, R0, L1, R1, L2, R2, bias, out):
         rrow1 = keep.tile([P, 256], F32)
         lrow = keep.tile([P, 224], F32)
         bias_sb = keep.tile([P, D], F32)
-        wc = keep.tile([P, 4 * HALF], U32, align_bytes=64)
-        ws = keep.tile([P, 4 * HALF], U8, align_bytes=64)
+        wc = keep.tile([P, 4 * HALF], U32, align_bytes=256)
+        ws = keep.tile([P, 4 * HALF], U8, align_bytes=256)
         xg = keep.tile([P, N_MACRO * 2048], BF16, align_bytes=64)
-        xc = keep.tile([P, N_MACRO * HALF], U32, align_bytes=64)
-        xs = keep.tile([P, N_MACRO * HALF], U8, align_bytes=64)
+        xc = keep.tile([P, 48 + N_MACRO * HALF], U32, align_bytes=256)
+        xs = keep.tile([P, 2 * N_MACRO * HALF], U8, align_bytes=256)
 
         nc.vector.memset(raw[:].bitcast(F32), 0.0)
         make_identity(nc, ident[:])
@@ -132,20 +132,21 @@ def tile_klinear_t_kernel(tc, x, L0, R0, L1, R1, L2, R2, bias, out):
                 )
 
         def x_quant(c):
-            nc.vector.quantize_mx(
-                out=xc[:, 1024 * c : 1024 * c + 1024].bitcast(FP8X4),
-                scales=xs[:, 1024 * c : 1024 * c + 1024],
-                in_=xg[:, 4096 * c : 4096 * c + 4096],
-            )
+            for o in range(8 * c, 8 * c + 8):
+                nc.vector.quantize_mx(
+                    out=xc[:, 48 + P * o : 48 + P * o + P].bitcast(FP8X4),
+                    scales=xs[:, 256 * o : 256 * o + P],
+                    in_=xg[:, HALF * o : HALF * o + HALF],
+                )
 
         def product(m, j, h):
             pb = psum.tile([P, HALF], F32, tag="bank")
             for g in range(2):
-                lo = HALF * m + 256 * j + P * g
+                o = 4 * m + 2 * j + g
                 nc.tensor.matmul_mx(
                     out=pb[:],
-                    lhsT=xc[:, lo : lo + P].bitcast(FP8X4),
-                    lhsT_scale=xs[:, lo : lo + P],
+                    lhsT=xc[:, 48 + P * o : 48 + P * o + P].bitcast(FP8X4),
+                    lhsT_scale=xs[:, 256 * o : 256 * o + P],
                     rhs=wc[:, HALF * (2 * h + g) : HALF * (2 * h + g) + HALF].bitcast(FP8X4),
                     rhs_scale=ws[:, HALF * (2 * h + g) : HALF * (2 * h + g) + HALF],
                     start=(g == 0),

@@ -12,11 +12,20 @@ MULT = mybir.AluOpType.mult
 ADD = mybir.AluOpType.add
 
 P = 128
+PACK = 4
 D = 1024
 HALF = 512
+PASSES = D // HALF
 TOKENS = 4096
 FLOPS = 2 * TOKENS * D * D
-N_MACRO = 16
+
+J = 2
+N_MACRO = TOKENS // (J * P)
+X_COLS = J * D
+X_WORDS = X_COLS // PACK
+PAIR = 2
+SLOT = 32
+
 EARLY = 5
 FIRST_T = 12
 QUANT_LEAD = 2
@@ -25,10 +34,13 @@ QUANT_LEAD = 2
 def tile_klinear_t_kernel(tc, x, L0, R0, L1, R1, L2, R2, bias, out):
     nc = tc.nc
     terms = [(L1, R1, 16, 64), (L0, R0, 32, 32), (L2, R2, 64, 16)]
-    r_off = [0, 256, 384]
-    l_off = [0, 32, 96]
-    xv = x.flatten_outer_dims().rearrange("(m p j) k -> m p (j k)", p=P, j=2)
-    ov = out.flatten_outer_dims().rearrange("(m p j) n -> m p j n", p=P, j=2)
+    r_off = [sum(PACK * t[3] for t in terms[:s]) for s in range(len(terms))]
+    l_off = [sum(PASSES * t[2] for t in terms[:s]) for s in range(len(terms))]
+    l_cols = sum(PASSES * t[2] for t in terms)
+    r1_cols = PACK * terms[0][3]
+    l_pad = 256
+    xv = x.flatten_outer_dims().rearrange("(m p j) k -> m p (j k)", p=P, j=J)
+    ov = out.flatten_outer_dims().rearrange("(m p j) n -> m p j n", p=P, j=J)
 
     with ExitStack() as ctx:
         keep = ctx.enter_context(tc.tile_pool(name="keep", bufs=1))
@@ -38,69 +50,69 @@ def tile_klinear_t_kernel(tc, x, L0, R0, L1, R1, L2, R2, bias, out):
         psum = ctx.enter_context(tc.psum_pool(name="psum", bufs=7))
         ctx.enter_context(tc.manual_schedule())
 
-        raw = keep.tile([P, 768], BF16)
+        raw = keep.tile([P, HALF + l_pad], BF16)
         rawb = keep.tile([P, D], BF16)
         ident = keep.tile([P, P], F32)
         sel1 = keep.tile([P, P], BF16)
         sel2 = keep.tile([P, P], BF16)
-        rrow1 = keep.tile([P, 256], F32)
-        lrow = keep.tile([P, 224], F32)
+        rrow1 = keep.tile([P, r1_cols], F32)
+        lrow = keep.tile([P, l_cols], F32)
         bias_sb = keep.tile([P, D], F32)
-        wc = keep.tile([P, 4 * HALF], U32, align_bytes=256)
-        ws = keep.tile([P, 4 * HALF], U8, align_bytes=256)
-        xg = keep.tile([P, N_MACRO * 2048], BF16, align_bytes=64)
-        xc = keep.tile([P, 48 + N_MACRO * HALF], U32, align_bytes=256)
-        xs = keep.tile([P, 2 * N_MACRO * HALF], U8, align_bytes=256)
+        wc = keep.tile([P, PASSES, D], U32, align_bytes=64)
+        ws = keep.tile([P, PASSES, D], U8, align_bytes=64)
+        xg = keep.tile([P, N_MACRO * X_COLS], BF16, align_bytes=64)
+        xc = keep.tile([P, N_MACRO * X_WORDS], U32, align_bytes=64)
+        xs = keep.tile([P, N_MACRO * X_WORDS], U8, align_bytes=64)
 
         nc.vector.memset(raw[:].bitcast(F32), 0.0)
         make_identity(nc, ident[:])
         for s, (lm, rm, np_, r) in enumerate(terms):
-            nq = r // 4
+            nq = r // PACK
+            nc.sync.dma_start(
+                out=raw[SLOT * s : SLOT * s + nq, r_off[s] : r_off[s] + PACK * r],
+                in_=rm.rearrange("(q t) d -> q (t d)", t=PACK),
+            )
+        for s, (lm, rm, np_, r) in enumerate(terms):
             ns = HALF // r
             nc.sync.dma_start(
-                out=raw[32 * s : 32 * s + nq, r_off[s] : r_off[s] + 4 * r],
-                in_=rm.rearrange("(q t) d -> q (t d)", t=4),
-            )
-            nc.sync.dma_start(
-                out=raw[32 * s : 32 * s + ns, HALF + l_off[s] : HALF + l_off[s] + 2 * np_].rearrange(
-                    "s (g b) -> s g b", g=2
+                out=raw[SLOT * s : SLOT * s + ns, HALF + l_off[s] : HALF + l_off[s] + PASSES * np_].rearrange(
+                    "s (g b) -> s g b", g=PASSES
                 ),
-                in_=lm.rearrange("(g s) b -> s g b", g=2),
+                in_=lm.rearrange("(g s) b -> s g b", g=PASSES),
             )
         nc.vector.memset(rawb[:].bitcast(F32), 0.0)
-        nc.sync.dma_start(out=rawb[96:97, :], in_=bias.unsqueeze(0))
+        nc.sync.dma_start(out=rawb[3 * SLOT : 3 * SLOT + 1, :], in_=bias.unsqueeze(0))
 
         for s, (lm, rm, np_, r) in enumerate(terms):
-            nq = r // 4
+            nq = r // PACK
             ns = HALF // r
-            rows = slice(32 * s, 32 * s + 32)
+            rows = slice(SLOT * s, SLOT * s + SLOT)
             nc.vector.tensor_copy(
                 out=sel1[rows, :].rearrange("k (a b) -> k a b", b=nq),
-                in_=ident[rows, 32 * s : 32 * s + nq].unsqueeze(1).to_broadcast([32, P // nq, nq]),
+                in_=ident[rows, SLOT * s : SLOT * s + nq].unsqueeze(1).to_broadcast([SLOT, P // nq, nq]),
             )
             nc.vector.tensor_copy(
                 out=sel2[rows, :].rearrange("k (a b) -> k a b", b=nq),
-                in_=ident[rows, 32 * s : 32 * s + ns].unsqueeze(2).to_broadcast([32, ns, nq]),
+                in_=ident[rows, SLOT * s : SLOT * s + ns].unsqueeze(2).to_broadcast([SLOT, ns, nq]),
             )
-        nc.vector.tensor_copy(out=sel1[96:128, :], in_=ident[96:128, 96:97].to_broadcast([32, P]))
-        nc.vector.memset(sel2[96:128, :], 0.0)
+        nc.vector.tensor_copy(
+            out=sel1[3 * SLOT : P, :], in_=ident[3 * SLOT : P, 3 * SLOT : 3 * SLOT + 1].to_broadcast([SLOT, P])
+        )
+        nc.vector.memset(sel2[3 * SLOT : P, :], 0.0)
 
         bank_r = psum_r.tile([P, HALF], F32)
-        nc.tensor.matmul(out=bank_r[:, 0:256], lhsT=sel1[:], rhs=raw[:, 0:256], start=True, stop=True)
-        bank_l1 = psum.tile([P, HALF], F32, tag="bank")
+        nc.tensor.matmul(out=bank_r[:], lhsT=sel1[:], rhs=raw[:, 0:HALF], start=True, stop=True)
+        bank_l = psum.tile([P, HALF], F32, tag="bank")
         nc.tensor.matmul(
-            out=bank_l1[:, 0:32], lhsT=sel2[:], rhs=raw[:, HALF : HALF + 32], start=True, stop=True
-        )
-        nc.vector.tensor_copy(
-            out=rrow1[:].rearrange("p (d t) -> p d t", t=4),
-            in_=bank_r[:, 0:256].rearrange("p (t d) -> p d t", t=4),
+            out=bank_l[:, 0:l_pad], lhsT=sel2[:], rhs=raw[:, HALF : HALF + l_pad], start=True, stop=True
         )
         nc.vector.tensor_scalar(
-            out=lrow[:, 0:32], in0=bank_l1[:, 0:32], scalar1=1.0 / 3.0, scalar2=None, op0=MULT
+            out=lrow[:], in0=bank_l[:, 0:l_cols], scalar1=1.0 / 3.0, scalar2=None, op0=MULT
         )
-        nc.tensor.matmul(out=bank_r[:, 256:HALF], lhsT=sel1[:], rhs=raw[:, 256:HALF], start=True, stop=True)
-        bank_l = psum.tile([P, HALF], F32, tag="bank")
-        nc.tensor.matmul(out=bank_l[:, 0:256], lhsT=sel2[:], rhs=raw[:, HALF:768], start=True, stop=True)
+        nc.vector.tensor_copy(
+            out=rrow1[:].rearrange("p (d t) -> p d t", t=PACK),
+            in_=bank_r[:, 0:r1_cols].rearrange("p (t d) -> p d t", t=PACK),
+        )
         for h in range(2):
             bank_b = psum.tile([P, HALF], F32, tag="bank")
             nc.tensor.matmul(
@@ -111,46 +123,45 @@ def tile_klinear_t_kernel(tc, x, L0, R0, L1, R1, L2, R2, bias, out):
         x_raw = {}
 
         def x_load(m):
-            xr = xpool.tile([P, 2048], BF16, tag="xr")
+            xr = xpool.tile([P, X_COLS], BF16, tag="xr")
             nc.sync.dma_start(out=xr[:], in_=xv[m])
             x_raw[m] = xr
 
         def x_transpose(m):
             xw = x_raw[m][:].bitcast(F32)
-            xgw = xg[:, 2048 * m : 2048 * m + 2048].bitcast(F32)
-            for j in range(2):
-                xt = psum.tile([P, 4, P], F32, tag="bank")
-                for g in range(2):
+            xgw = xg[:, X_COLS * m : X_COLS * m + X_COLS].bitcast(F32)
+            for j in range(J):
+                xt = psum.tile([P, 2 * PASSES, P], F32, tag="bank")
+                for g in range(PASSES):
                     words = xw[:, HALF * j + 256 * g : HALF * j + 256 * g + 256].rearrange(
                         "m (p u) -> m u p", u=2
                     )
                     for u in range(2):
                         nc.tensor.transpose(xt[:, 2 * g + u, :], words[:, u, :], ident[:])
                 nc.scalar.copy(
-                    out=xgw[:, HALF * j : HALF * j + HALF].rearrange("p (g m u) -> p g m u", g=2, u=2),
+                    out=xgw[:, HALF * j : HALF * j + HALF].rearrange("p (g m u) -> p g m u", g=PASSES, u=2),
                     in_=xt[:].rearrange("p (g u) m -> p g m u", u=2),
                 )
 
         def x_quant(c):
-            for o in range(8 * c, 8 * c + 8):
-                nc.vector.quantize_mx(
-                    out=xc[:, 48 + P * o : 48 + P * o + P].bitcast(FP8X4),
-                    scales=xs[:, 256 * o : 256 * o + P],
-                    in_=xg[:, HALF * o : HALF * o + HALF],
-                )
+            nc.vector.quantize_mx(
+                out=xc[:, PAIR * X_WORDS * c : PAIR * X_WORDS * (c + 1)].bitcast(FP8X4),
+                scales=xs[:, PAIR * X_WORDS * c : PAIR * X_WORDS * (c + 1)],
+                in_=xg[:, PAIR * X_COLS * c : PAIR * X_COLS * (c + 1)],
+            )
 
         def product(m, j, h):
             pb = psum.tile([P, HALF], F32, tag="bank")
-            for g in range(2):
-                o = 4 * m + 2 * j + g
+            for g in range(PASSES):
+                lo = X_WORDS * m + PASSES * P * j + P * g
                 nc.tensor.matmul_mx(
                     out=pb[:],
-                    lhsT=xc[:, 48 + P * o : 48 + P * o + P].bitcast(FP8X4),
-                    lhsT_scale=xs[:, 256 * o : 256 * o + P],
-                    rhs=wc[:, HALF * (2 * h + g) : HALF * (2 * h + g) + HALF].bitcast(FP8X4),
-                    rhs_scale=ws[:, HALF * (2 * h + g) : HALF * (2 * h + g) + HALF],
+                    lhsT=xc[:, lo : lo + P].bitcast(FP8X4),
+                    lhsT_scale=xs[:, lo : lo + P],
+                    rhs=wc[:, g, HALF * h : HALF * h + HALF].bitcast(FP8X4),
+                    rhs_scale=ws[:, g, HALF * h : HALF * h + HALF],
                     start=(g == 0),
-                    stop=(g == 1),
+                    stop=(g == PASSES - 1),
                 )
             return pb
 
@@ -163,8 +174,8 @@ def tile_klinear_t_kernel(tc, x, L0, R0, L1, R1, L2, R2, bias, out):
                 nc.vector.tensor_tensor(out=dst, in0=pb[:], in1=bs, op=ADD)
 
         def half_rows(pool, tag, m, h, n_scalar):
-            oh = pool.tile([P, 2, HALF], F32, tag=tag, name=tag)
-            for j in range(2):
+            oh = pool.tile([P, J, HALF], F32, tag=tag, name=tag)
+            for j in range(J):
                 leave(product(m, j, h), oh[:, j, :], h, j < n_scalar)
             nc.sync.dma_start(out=ov[m][:, :, HALF * h : HALF * h + HALF], in_=oh[:])
 
@@ -173,17 +184,15 @@ def tile_klinear_t_kernel(tc, x, L0, R0, L1, R1, L2, R2, bias, out):
             x_transpose(m)
 
         with tc.tile_pool(name="wpool", bufs=1) as wpool:
-            acc = wpool.tile([P, 8 * D], F32)
-            wbf = wpool.tile([P, 8 * D], BF16, align_bytes=64)
+            acc = wpool.tile([P, PASSES, PACK * D], F32)
+            wbf = wpool.tile([P, PASSES, PACK * D], BF16, align_bytes=64)
 
             def w_term(s, h, g, first=0, last=None, on_gpsimd=False):
                 lm, rm, np_, r = terms[s]
-                w = 4 * r
-                for i in list(range(np_ // 2))[first:last]:
-                    b = h * np_ // 2 + i
+                w = PACK * r
+                for b in list(range(h * np_ // 2, (h + 1) * np_ // 2))[first:last]:
                     sc = lrow[:, l_off[s] + g * np_ + b : l_off[s] + g * np_ + b + 1]
-                    lo = 2048 * (2 * h + g) + w * i
-                    dst = acc[:, lo : lo + w]
+                    dst = acc[:, g, w * b : w * b + w]
                     if s == 0 and on_gpsimd:
                         nc.gpsimd.tensor_scalar(
                             out=dst, in0=rrow1[:], scalar1=sc, scalar2=0.0, op0=MULT, op1=ADD
@@ -191,65 +200,63 @@ def tile_klinear_t_kernel(tc, x, L0, R0, L1, R1, L2, R2, bias, out):
                     elif s == 0:
                         nc.vector.tensor_scalar(out=dst, in0=rrow1[:], scalar1=sc, scalar2=None, op0=MULT)
                     else:
-                        res = dst if s == 1 else wbf[:, lo : lo + w]
+                        res = dst if s == 1 else wbf[:, g, w * b : w * b + w]
                         nc.vector.scalar_tensor_tensor(
-                            out=res.rearrange("p (d t) -> p d t", t=4),
-                            in0=bank_r[:, r_off[s] : r_off[s] + w].rearrange("p (t d) -> p d t", t=4),
+                            out=res.rearrange("p (d t) -> p d t", t=PACK),
+                            in0=bank_r[:, r_off[s] : r_off[s] + w].rearrange("p (t d) -> p d t", t=PACK),
                             scalar=sc,
-                            in1=dst.rearrange("p (d t) -> p d t", t=4),
+                            in1=dst.rearrange("p (d t) -> p d t", t=PACK),
                             op0=MULT,
                             op1=ADD,
                         )
 
-            def w_quant(h):
+            def w_quant(h, g):
                 nc.vector.quantize_mx(
-                    out=wc[:, D * h : D * h + D].bitcast(FP8X4),
-                    scales=ws[:, D * h : D * h + D],
-                    in_=wbf[:, 4 * D * h : 4 * D * h + 4 * D],
+                    out=wc[:, g, HALF * h : HALF * h + HALF].bitcast(FP8X4),
+                    scales=ws[:, g, HALF * h : HALF * h + HALF],
+                    in_=wbf[:, g, PACK * HALF * h : PACK * HALF * (h + 1)],
                 )
 
             w_term(0, 0, 0)
-            nc.vector.tensor_scalar(
-                out=lrow[:, 32:224], in0=bank_l[:, 32:224], scalar1=1.0 / 3.0, scalar2=None, op0=MULT
-            )
             w_term(0, 0, 1, on_gpsimd=True)
             w_term(0, 1, 0, on_gpsimd=True)
             w_term(0, 1, 1, on_gpsimd=True)
-            for g in range(2):
+            for g in range(PASSES):
                 w_term(1, 0, g)
                 w_term(2, 0, g)
+            w_quant(0, 0)
             w_term(1, 1, 0, last=4)
-            w_quant(0)
-            for c in range((EARLY + 1) // 2):
+            w_quant(0, 1)
+            for c in range((EARLY + 1) // PAIR):
                 x_quant(c)
             for m in range(FIRST_T, N_MACRO):
                 x_load(m)
             for e in range(EARLY):
-                half_rows(hpool, "oh", e, 0, 2)
+                half_rows(hpool, "oh", e, 0, J)
                 if FIRST_T + e < N_MACRO:
                     x_transpose(FIRST_T + e)
             w_term(1, 1, 0, first=4)
             w_term(2, 1, 0)
             w_term(1, 1, 1)
+            w_quant(1, 0)
             w_term(2, 1, 1)
-            w_quant(1)
+            w_quant(1, 1)
 
         opool = ctx.enter_context(tc.tile_pool(name="opool", bufs=6))
         for m in range(N_MACRO):
-            c = (m + QUANT_LEAD) // 2
-            if (m + QUANT_LEAD) % 2 == 0 and (EARLY + 1) // 2 <= c < N_MACRO // 2:
+            c = (m + QUANT_LEAD) // PAIR
+            if (m + QUANT_LEAD) % PAIR == 0 and (EARLY + 1) // PAIR <= c < N_MACRO // PAIR:
                 x_quant(c)
             if m < EARLY:
                 half_rows(opool, "ot", m, 1, 1 - m % 2)
                 continue
             last = m == N_MACRO - 1
-            ot = opool.tile([P, 2, D], F32, tag="ot")
-            for j in range(2):
+            ot = opool.tile([P, J, D], F32, tag="ot")
+            for j in range(J):
                 for h in range(2):
                     by_scalar = j == 0 and h == 0 and not last
-                    cols = slice(HALF * h, HALF * h + HALF)
-                    leave(product(m, j, h), ot[:, j, cols], h, by_scalar)
-                    if last:
-                        nc.sync.dma_start(out=ov[m][:, j, cols], in_=ot[:, j, cols])
+                    leave(product(m, j, h), ot[:, j, HALF * h : HALF * h + HALF], h, by_scalar)
+                if last:
+                    nc.sync.dma_start(out=ov[m][:, j, :], in_=ot[:, j, :])
             if not last:
                 nc.sync.dma_start(out=ov[m], in_=ot[:])

@@ -227,18 +227,26 @@ def tile_klinear_t_kernel(tc, x, L0, R0, L1, R1, L2, R2, bias, out):
             w_quant(0, 0)
             w_term(1, 1, 0, last=4)
             w_quant(0, 1)
-            for c in range((EARLY + 1) // PAIR):
-                x_quant(c)
+            x_quant(0)
             for m in range(FIRST_T, N_MACRO):
                 x_load(m)
-            for e in range(EARLY):
+
+            def early(e):
                 half_rows(hpool, "oh", e, 0, J)
                 if FIRST_T + e < N_MACRO:
                     x_transpose(FIRST_T + e)
+
+            early(0)
+            early(1)
             w_term(1, 1, 0, first=4)
             w_term(2, 1, 0)
+            x_quant(1)
+            early(2)
+            early(3)
             w_term(1, 1, 1)
             w_quant(1, 0)
+            x_quant(2)
+            early(4)
             w_term(2, 1, 1)
             w_quant(1, 1)
 

@@ -26,9 +26,12 @@ X_WORDS = X_COLS // PACK
 PAIR = 2
 SLOT = 32
 
-EARLY = 5
+EARLY = 6
 FIRST_T = 12
 QUANT_LEAD = 2
+LATE_FROM = 4
+LATE_AFTER = (2, 4)
+R_SCALAR = (0, 0, 0, 0, 1, 1)
 
 
 def tile_klinear_t_kernel(tc, x, L0, R0, L1, R1, L2, R2, bias, out):
@@ -173,10 +176,19 @@ def tile_klinear_t_kernel(tc, x, L0, R0, L1, R1, L2, R2, bias, out):
             else:
                 nc.vector.tensor_tensor(out=dst, in0=pb[:], in1=bs, op=ADD)
 
-        def half_rows(pool, tag, m, h, n_scalar):
+        late_stores = []
+
+        def half_rows(pool, tag, m, h, n_scalar, store_later=False):
             oh = pool.tile([P, J, HALF], F32, tag=tag, name=tag)
             for j in range(J):
                 leave(product(m, j, h), oh[:, j, :], h, j < n_scalar)
+            if store_later:
+                late_stores.append((m, h, oh))
+            else:
+                nc.sync.dma_start(out=ov[m][:, :, HALF * h : HALF * h + HALF], in_=oh[:])
+
+        def store_late():
+            m, h, oh = late_stores.pop(0)
             nc.sync.dma_start(out=ov[m][:, :, HALF * h : HALF * h + HALF], in_=oh[:])
 
         for m in range(FIRST_T):
@@ -232,21 +244,24 @@ def tile_klinear_t_kernel(tc, x, L0, R0, L1, R1, L2, R2, bias, out):
                 x_load(m)
 
             def early(e):
-                half_rows(hpool, "oh", e, 0, J)
-                if FIRST_T + e < N_MACRO:
-                    x_transpose(FIRST_T + e)
+                half_rows(hpool, "oh", e, 0, J, store_later=e >= LATE_FROM)
 
             early(0)
             early(1)
+            x_transpose(12)
+            x_transpose(13)
             w_term(1, 1, 0, first=4)
             w_term(2, 1, 0)
             x_quant(1)
             early(2)
             early(3)
+            x_transpose(14)
+            x_transpose(15)
             w_term(1, 1, 1)
             w_quant(1, 0)
             x_quant(2)
             early(4)
+            early(5)
             w_term(2, 1, 1)
             w_quant(1, 1)
 
@@ -256,7 +271,9 @@ def tile_klinear_t_kernel(tc, x, L0, R0, L1, R1, L2, R2, bias, out):
             if (m + QUANT_LEAD) % PAIR == 0 and (EARLY + 1) // PAIR <= c < N_MACRO // PAIR:
                 x_quant(c)
             if m < EARLY:
-                half_rows(opool, "ot", m, 1, 1 - m % 2)
+                half_rows(opool, "ot", m, 1, R_SCALAR[m])
+                if m in LATE_AFTER:
+                    store_late()
                 continue
             last = m == N_MACRO - 1
             ot = opool.tile([P, J, D], F32, tag="ot")

@@ -67,7 +67,20 @@ def tile_klinear_t_kernel(tc, x, L0, R0, L1, R1, L2, R2, bias, out):
         xc = keep.tile([P, N_MACRO * X_WORDS], U32, align_bytes=64)
         xs = keep.tile([P, N_MACRO * X_WORDS], U8, align_bytes=64)
 
-        nc.vector.memset(raw[:].bitcast(F32), 0.0)
+        x_raw = {}
+
+        def x_load(m, parts=1):
+            if m not in x_raw:
+                xr = xpool.tile([P, X_COLS], BF16, tag="xr")
+                x_raw[m] = xr
+                cols = slice(0, X_COLS // parts)
+            else:
+                cols = slice(D, X_COLS)
+            nc.sync.dma_start(out=x_raw[m][:, cols], in_=xv[m][:, cols])
+
+        x_load(0, parts=J)
+
+        nc.gpsimd.memset(raw[:].bitcast(F32), 0.0)
         make_identity(nc, ident[:])
         for s, (lm, rm, np_, r) in enumerate(terms):
             nq = r // PACK
@@ -112,7 +125,7 @@ def tile_klinear_t_kernel(tc, x, L0, R0, L1, R1, L2, R2, bias, out):
         nc.vector.tensor_scalar(
             out=lrow[:], in0=bank_l[:, 0:l_cols], scalar1=1.0 / 3.0, scalar2=None, op0=MULT
         )
-        nc.vector.tensor_copy(
+        nc.scalar.copy(
             out=rrow1[:].rearrange("p (d t) -> p d t", t=PACK),
             in_=bank_r[:, 0:r1_cols].rearrange("p (t d) -> p d t", t=PACK),
         )
@@ -122,13 +135,6 @@ def tile_klinear_t_kernel(tc, x, L0, R0, L1, R1, L2, R2, bias, out):
                 out=bank_b[:], lhsT=sel1[:], rhs=rawb[:, HALF * h : HALF * h + HALF], start=True, stop=True
             )
             nc.scalar.copy(out=bias_sb[:, HALF * h : HALF * h + HALF], in_=bank_b[:])
-
-        x_raw = {}
-
-        def x_load(m):
-            xr = xpool.tile([P, X_COLS], BF16, tag="xr")
-            nc.sync.dma_start(out=xr[:], in_=xv[m])
-            x_raw[m] = xr
 
         def x_transpose(m):
             xw = x_raw[m][:].bitcast(F32)
@@ -251,17 +257,18 @@ def tile_klinear_t_kernel(tc, x, L0, R0, L1, R1, L2, R2, bias, out):
             x_transpose(12)
             x_transpose(13)
             w_term(1, 1, 0, first=4)
-            w_term(2, 1, 0)
+            w_term(2, 1, 0, last=16)
             x_quant(1)
             early(2)
             early(3)
             x_transpose(14)
             x_transpose(15)
+            w_term(2, 1, 0, first=16)
             w_term(1, 1, 1)
-            w_quant(1, 0)
             x_quant(2)
             early(4)
             early(5)
+            w_quant(1, 0)
             w_term(2, 1, 1)
             w_quant(1, 1)
 

@@ -16,6 +16,7 @@ PACK = 4
 D = 1024
 HALF = 512
 PASSES = D // HALF
+ROWS = PASSES * PACK
 TOKENS = 4096
 FLOPS = 2 * TOKENS * D * D
 
@@ -32,16 +33,20 @@ QUANT_LEAD = 2
 LATE_FROM = 4
 LATE_AFTER = (2, 4)
 R_SCALAR = (0, 0, 0, 0, 1, 1)
+V_FIRST = 1
+N_BLOCKS = 8
 
 
 def tile_klinear_t_kernel(tc, x, L0, R0, L1, R1, L2, R2, bias, out):
     nc = tc.nc
     terms = [(L1, R1, 16, 64), (L0, R0, 32, 32), (L2, R2, 64, 16)]
-    r_off = [sum(PACK * t[3] for t in terms[:s]) for s in range(len(terms))]
-    l_off = [sum(PASSES * t[2] for t in terms[:s]) for s in range(len(terms))]
-    l_cols = sum(PASSES * t[2] for t in terms)
-    r1_cols = PACK * terms[0][3]
-    l_pad = 256
+    r_off = [sum(ROWS * t[3] for t in terms[:s]) for s in range(len(terms))]
+    l_off = [sum(t[2] for t in terms[:s]) for s in range(len(terms))]
+    r_cols = sum(ROWS * t[3] for t in terms)
+    l_cols = sum(t[2] for t in terms)
+    r1_cols = ROWS * terms[0][3]
+    l_pad = 128
+    l_base = (96, 64, 0)
     xv = x.flatten_outer_dims().rearrange("(m p j) k -> m p (j k)", p=P, j=J)
     ov = out.flatten_outer_dims().rearrange("(m p j) n -> m p j n", p=P, j=J)
 
@@ -53,7 +58,7 @@ def tile_klinear_t_kernel(tc, x, L0, R0, L1, R1, L2, R2, bias, out):
         psum = ctx.enter_context(tc.psum_pool(name="psum", bufs=7))
         ctx.enter_context(tc.manual_schedule())
 
-        raw = keep.tile([P, HALF + l_pad], BF16)
+        raw = keep.tile([P, r_cols + l_pad], BF16)
         rawb = keep.tile([P, D], BF16)
         ident = keep.tile([P, P], F32)
         sel1 = keep.tile([P, P], BF16)
@@ -83,52 +88,59 @@ def tile_klinear_t_kernel(tc, x, L0, R0, L1, R1, L2, R2, bias, out):
         nc.gpsimd.memset(raw[:].bitcast(F32), 0.0)
         make_identity(nc, ident[:])
         for s, (lm, rm, np_, r) in enumerate(terms):
-            nq = r // PACK
+            nq = r // ROWS
             nc.sync.dma_start(
-                out=raw[SLOT * s : SLOT * s + nq, r_off[s] : r_off[s] + PACK * r],
-                in_=rm.rearrange("(q t) d -> q (t d)", t=PACK),
+                out=raw[SLOT * s : SLOT * s + nq, r_off[s] : r_off[s] + ROWS * r],
+                in_=rm.rearrange("(q t) d -> q (t d)", t=ROWS),
             )
         for s, (lm, rm, np_, r) in enumerate(terms):
-            ns = HALF // r
             nc.sync.dma_start(
-                out=raw[SLOT * s : SLOT * s + ns, HALF + l_off[s] : HALF + l_off[s] + PASSES * np_].rearrange(
-                    "s (g b) -> s g b", g=PASSES
-                ),
-                in_=lm.rearrange("(g s) b -> s g b", g=PASSES),
+                out=raw[l_base[s] : l_base[s] + np_, r_cols + l_off[s] : r_cols + l_off[s] + np_], in_=lm
             )
         nc.vector.memset(rawb[:].bitcast(F32), 0.0)
         nc.sync.dma_start(out=rawb[3 * SLOT : 3 * SLOT + 1, :], in_=bias.unsqueeze(0))
 
         for s, (lm, rm, np_, r) in enumerate(terms):
-            nq = r // PACK
-            ns = HALF // r
+            nq = r // ROWS
             rows = slice(SLOT * s, SLOT * s + SLOT)
             nc.vector.tensor_copy(
                 out=sel1[rows, :].rearrange("k (a b) -> k a b", b=nq),
                 in_=ident[rows, SLOT * s : SLOT * s + nq].unsqueeze(1).to_broadcast([SLOT, P // nq, nq]),
             )
+            n_rows = max(np_, SLOT)
+            rows = slice(l_base[s], l_base[s] + n_rows)
             nc.vector.tensor_copy(
                 out=sel2[rows, :].rearrange("k (a b) -> k a b", b=nq),
-                in_=ident[rows, SLOT * s : SLOT * s + ns].unsqueeze(2).to_broadcast([SLOT, ns, nq]),
+                in_=ident[rows, l_base[s] : l_base[s] + np_].unsqueeze(2).to_broadcast([n_rows, np_, nq]),
             )
         nc.vector.tensor_copy(
             out=sel1[3 * SLOT : P, :], in_=ident[3 * SLOT : P, 3 * SLOT : 3 * SLOT + 1].to_broadcast([SLOT, P])
         )
-        nc.vector.memset(sel2[3 * SLOT : P, :], 0.0)
 
-        bank_r = psum_r.tile([P, HALF], F32)
-        nc.tensor.matmul(out=bank_r[:], lhsT=sel1[:], rhs=raw[:, 0:HALF], start=True, stop=True)
+        def select_r(bank, lo, s):
+            w = PACK * terms[s][3]
+            for g in range(PASSES):
+                nc.tensor.matmul(
+                    out=bank[:, lo + w * g : lo + w * (g + 1)].rearrange("p (d t) -> p d t", t=PACK),
+                    lhsT=sel1[:],
+                    rhs=raw[:, r_off[s] + w * g : r_off[s] + w * (g + 1)].rearrange("k (t d) -> k d t", t=PACK),
+                    start=True,
+                    stop=True,
+                )
+
+        bank_r1 = psum.tile([P, HALF], F32, tag="bank")
+        select_r(bank_r1, 0, 0)
         bank_l = psum.tile([P, HALF], F32, tag="bank")
         nc.tensor.matmul(
-            out=bank_l[:, 0:l_pad], lhsT=sel2[:], rhs=raw[:, HALF : HALF + l_pad], start=True, stop=True
+            out=bank_l[:, 0:l_pad], lhsT=sel2[:], rhs=raw[:, r_cols : r_cols + l_pad], start=True, stop=True
         )
+        bank_r = psum_r.tile([P, HALF], F32)
+        for s in range(1, len(terms)):
+            select_r(bank_r, r_off[s] - r1_cols, s)
         nc.vector.tensor_scalar(
             out=lrow[:], in0=bank_l[:, 0:l_cols], scalar1=1.0 / 3.0, scalar2=None, op0=MULT
         )
-        nc.scalar.copy(
-            out=rrow1[:].rearrange("p (d t) -> p d t", t=PACK),
-            in_=bank_r[:, 0:r1_cols].rearrange("p (t d) -> p d t", t=PACK),
-        )
+        nc.scalar.copy(out=rrow1[:], in_=bank_r1[:])
         for h in range(2):
             bank_b = psum.tile([P, HALF], F32, tag="bank")
             nc.tensor.matmul(
@@ -141,12 +153,9 @@ def tile_klinear_t_kernel(tc, x, L0, R0, L1, R1, L2, R2, bias, out):
             xgw = xg[:, X_COLS * m : X_COLS * m + X_COLS].bitcast(F32)
             for j in range(J):
                 xt = psum.tile([P, 2 * PASSES, P], F32, tag="bank")
-                for g in range(PASSES):
-                    words = xw[:, HALF * j + 256 * g : HALF * j + 256 * g + 256].rearrange(
-                        "m (p u) -> m u p", u=2
-                    )
-                    for u in range(2):
-                        nc.tensor.transpose(xt[:, 2 * g + u, :], words[:, u, :], ident[:])
+                words = xw[:, HALF * j : HALF * j + HALF].rearrange("m (p q) -> m q p", q=2 * PASSES)
+                for q in range(2 * PASSES):
+                    nc.tensor.transpose(xt[:, q, :], words[:, q, :], ident[:])
                 nc.scalar.copy(
                     out=xgw[:, HALF * j : HALF * j + HALF].rearrange("p (g m u) -> p g m u", g=PASSES, u=2),
                     in_=xt[:].rearrange("p (g u) m -> p g m u", u=2),
@@ -186,8 +195,14 @@ def tile_klinear_t_kernel(tc, x, L0, R0, L1, R1, L2, R2, bias, out):
 
         def half_rows(pool, tag, m, h, n_scalar, store_later=False):
             oh = pool.tile([P, J, HALF], F32, tag=tag, name=tag)
-            for j in range(J):
-                leave(product(m, j, h), oh[:, j, :], h, j < n_scalar)
+            if n_scalar == J:
+                for j in range(J):
+                    nc.scalar.copy(out=oh[:, j, :], in_=product(m, j, h)[:])
+                bs = bias_sb[:, HALF * h : HALF * h + HALF].unsqueeze(1).to_broadcast([P, J, HALF])
+                nc.gpsimd.tensor_tensor(out=oh[:], in0=oh[:], in1=bs, op=ADD)
+            else:
+                for j in range(J):
+                    leave(product(m, j, h), oh[:, j, :], h, j < n_scalar)
             if store_later:
                 late_stores.append((m, h, oh))
             else:
@@ -202,49 +217,54 @@ def tile_klinear_t_kernel(tc, x, L0, R0, L1, R1, L2, R2, bias, out):
             x_transpose(m)
 
         with tc.tile_pool(name="wpool", bufs=1) as wpool:
-            acc = wpool.tile([P, PASSES, PACK * D], F32)
+            w1 = PACK * terms[0][3]
+            acc = wpool.tile([P, terms[0][2], PASSES, w1], F32)
             wbf = wpool.tile([P, PASSES, PACK * D], BF16, align_bytes=64)
 
-            def w_term(s, h, g, first=0, last=None, on_gpsimd=False):
+            def w_term(s, h, first=0, last=None, on_gpsimd=False):
                 lm, rm, np_, r = terms[s]
                 w = PACK * r
+                row1 = rrow1[:].rearrange("p (g c) -> p g c", g=PASSES)
                 for b in list(range(h * np_ // 2, (h + 1) * np_ // 2))[first:last]:
-                    sc = lrow[:, l_off[s] + g * np_ + b : l_off[s] + g * np_ + b + 1]
-                    dst = acc[:, g, w * b : w * b + w]
+                    sc = lrow[:, l_off[s] + b : l_off[s] + b + 1]
+                    dst = acc[:, w * b // w1, :, w * b % w1 : w * b % w1 + w]
                     if s == 0 and on_gpsimd:
-                        nc.gpsimd.tensor_scalar(
-                            out=dst, in0=rrow1[:], scalar1=sc, scalar2=0.0, op0=MULT, op1=ADD
-                        )
+                        nc.gpsimd.tensor_scalar(out=dst, in0=row1, scalar1=sc, scalar2=0.0, op0=MULT, op1=ADD)
                     elif s == 0:
-                        nc.vector.tensor_scalar(out=dst, in0=rrow1[:], scalar1=sc, scalar2=None, op0=MULT)
+                        nc.vector.tensor_scalar(out=dst, in0=row1, scalar1=sc, scalar2=None, op0=MULT)
                     else:
-                        res = dst if s == 1 else wbf[:, g, w * b : w * b + w]
+                        res = dst if s == 1 else wbf[:, :, w * b : w * b + w]
+                        lo = r_off[s] - r1_cols
                         nc.vector.scalar_tensor_tensor(
-                            out=res.rearrange("p (d t) -> p d t", t=PACK),
-                            in0=bank_r[:, r_off[s] : r_off[s] + w].rearrange("p (t d) -> p d t", t=PACK),
+                            out=res,
+                            in0=bank_r[:, lo : lo + ROWS * r].rearrange("p (g c) -> p g c", g=PASSES),
                             scalar=sc,
-                            in1=dst.rearrange("p (d t) -> p d t", t=PACK),
+                            in1=dst,
                             op0=MULT,
                             op1=ADD,
                         )
 
-            def w_quant(h, g):
+            def w_quant(g, lo, n):
                 nc.vector.quantize_mx(
-                    out=wc[:, g, HALF * h : HALF * h + HALF].bitcast(FP8X4),
-                    scales=ws[:, g, HALF * h : HALF * h + HALF],
-                    in_=wbf[:, g, PACK * HALF * h : PACK * HALF * (h + 1)],
+                    out=wc[:, g, lo : lo + n].bitcast(FP8X4),
+                    scales=ws[:, g, lo : lo + n],
+                    in_=wbf[:, g, PACK * lo : PACK * (lo + n)],
                 )
 
-            w_term(0, 0, 0)
-            w_term(0, 0, 1, on_gpsimd=True)
-            w_term(0, 1, 0, on_gpsimd=True)
-            w_term(0, 1, 1, on_gpsimd=True)
+            w_term(0, 0, last=V_FIRST)
+            w_term(0, 0, first=V_FIRST, on_gpsimd=True)
+            w_term(0, 1, on_gpsimd=True)
+
+            def w_rest(h, lo, hi):
+                for s in range(1, len(terms)):
+                    per = terms[s][2] // terms[0][2]
+                    w_term(s, h, first=per * lo, last=per * hi)
+
+            for lo in range(0, N_BLOCKS, 2):
+                w_rest(0, lo, lo + 2)
+            w_rest(1, 0, 1)
             for g in range(PASSES):
-                w_term(1, 0, g)
-                w_term(2, 0, g)
-            w_quant(0, 0)
-            w_term(1, 1, 0, last=4)
-            w_quant(0, 1)
+                w_quant(g, 0, HALF)
             x_quant(0)
             for m in range(FIRST_T, N_MACRO):
                 x_load(m)
@@ -256,21 +276,20 @@ def tile_klinear_t_kernel(tc, x, L0, R0, L1, R1, L2, R2, bias, out):
             early(1)
             x_transpose(12)
             x_transpose(13)
-            w_term(1, 1, 0, first=4)
-            w_term(2, 1, 0, last=16)
+            w_rest(1, 1, 3)
             x_quant(1)
             early(2)
             early(3)
             x_transpose(14)
             x_transpose(15)
-            w_term(2, 1, 0, first=16)
-            w_term(1, 1, 1)
+            w_rest(1, 3, 6)
             x_quant(2)
             early(4)
             early(5)
-            w_quant(1, 0)
-            w_term(2, 1, 1)
-            w_quant(1, 1)
+            w_rest(1, 6, N_BLOCKS)
+            for lo in (HALF, HALF + HALF // 2):
+                for g in range(PASSES):
+                    w_quant(g, lo, HALF // 2)
 
         opool = ctx.enter_context(tc.tile_pool(name="opool", bufs=6))
         for m in range(N_MACRO):

@@ -266,6 +266,8 @@ def tile_klinear_t_kernel(tc, x, L0, R0, L1, R1, L2, R2, bias, out):
             for g in range(PASSES):
                 w_quant(g, 0, HALF)
             x_quant(0)
+            x_quant(1)
+            x_quant(2)
             for m in range(FIRST_T, N_MACRO):
                 x_load(m)
 
@@ -277,13 +279,11 @@ def tile_klinear_t_kernel(tc, x, L0, R0, L1, R1, L2, R2, bias, out):
             x_transpose(12)
             x_transpose(13)
             w_rest(1, 1, 3)
-            x_quant(1)
             early(2)
             early(3)
             x_transpose(14)
             x_transpose(15)
             w_rest(1, 3, 6)
-            x_quant(2)
             early(4)
             early(5)
             w_rest(1, 6, N_BLOCKS)

@@ -275,13 +275,13 @@ def tile_klinear_t_kernel(tc, x, L0, R0, L1, R1, L2, R2, bias, out):
                 half_rows(hpool, "oh", e, 0, J, store_later=e >= LATE_FROM)
 
             early(0)
-            early(1)
             x_transpose(12)
+            early(1)
             x_transpose(13)
             w_rest(1, 1, 3)
             early(2)
-            early(3)
             x_transpose(14)
+            early(3)
             x_transpose(15)
             w_rest(1, 3, 6)
             early(4)

from contextlib import ExitStack

import concourse.mybir as mybir
from concourse.masks import make_identity

F32 = mybir.dt.float32
BF16 = mybir.dt.bfloat16
U32 = mybir.dt.uint32
U8 = mybir.dt.uint8
FP8X4 = mybir.dt.float8_e4m3fn_x4
MULT = mybir.AluOpType.mult
ADD = mybir.AluOpType.add

P = 128
PACK = 4
D = 1024
HALF = 512
PASSES = D // HALF
ROWS = PASSES * PACK
TOKENS = 4096
FLOPS = 2 * TOKENS * D * D

J = 2
N_MACRO = TOKENS // (J * P)
X_COLS = J * D
X_WORDS = X_COLS // PACK
PAIR = 2
SLOT = 32

EARLY = 6
FIRST_T = 12
QUANT_LEAD = 2
LATE_FROM = 4
LATE_AFTER = (2, 4)
R_SCALAR = (0, 0, 0, 0, 1, 1)
V_FIRST = 1
N_BLOCKS = 8


def tile_klinear_t_kernel(tc, x, L0, R0, L1, R1, L2, R2, bias, out):
    nc = tc.nc
    terms = [(L1, R1, 16, 64), (L0, R0, 32, 32), (L2, R2, 64, 16)]
    r_off = [sum(ROWS * t[3] for t in terms[:s]) for s in range(len(terms))]
    l_off = [sum(t[2] for t in terms[:s]) for s in range(len(terms))]
    r_cols = sum(ROWS * t[3] for t in terms)
    l_cols = sum(t[2] for t in terms)
    r1_cols = ROWS * terms[0][3]
    l_pad = 128
    l_base = (96, 64, 0)
    xv = x.flatten_outer_dims().rearrange("(m p j) k -> m p (j k)", p=P, j=J)
    ov = out.flatten_outer_dims().rearrange("(m p j) n -> m p j n", p=P, j=J)

    with ExitStack() as ctx:
        keep = ctx.enter_context(tc.tile_pool(name="keep", bufs=1))
        xpool = ctx.enter_context(tc.tile_pool(name="xpool", bufs=4))
        hpool = ctx.enter_context(tc.tile_pool(name="hpool", bufs=4))
        psum_r = ctx.enter_context(tc.psum_pool(name="psum_r", bufs=1))
        psum = ctx.enter_context(tc.psum_pool(name="psum", bufs=7))
        ctx.enter_context(tc.manual_schedule())

        raw = keep.tile([P, r_cols + l_pad], BF16)
        rawb = keep.tile([P, D], BF16)
        ident = keep.tile([P, P], F32)
        sel1 = keep.tile([P, P], BF16)
        sel2 = keep.tile([P, P], BF16)
        rrow1 = keep.tile([P, r1_cols], F32)
        lrow = keep.tile([P, l_cols], F32)
        bias_sb = keep.tile([P, D], F32)
        wc = keep.tile([P, PASSES, D], U32, align_bytes=64)
        ws = keep.tile([P, PASSES, D], U8, align_bytes=64)
        xg = keep.tile([P, N_MACRO * X_COLS], BF16, align_bytes=64)
        xc = keep.tile([P, N_MACRO * X_WORDS], U32, align_bytes=64)
        xs = keep.tile([P, N_MACRO * X_WORDS], U8, align_bytes=64)

        x_raw = {}

        def x_load(m, parts=1):
            if m not in x_raw:
                xr = xpool.tile([P, X_COLS], BF16, tag="xr")
                x_raw[m] = xr
                cols = slice(0, X_COLS // parts)
            else:
                cols = slice(D, X_COLS)
            nc.sync.dma_start(out=x_raw[m][:, cols], in_=xv[m][:, cols])

        x_load(0, parts=J)

        nc.gpsimd.memset(raw[:].bitcast(F32), 0.0)
        make_identity(nc, ident[:])
        for s, (lm, rm, np_, r) in enumerate(terms):
            nq = r // ROWS
            nc.sync.dma_start(
                out=raw[SLOT * s : SLOT * s + nq, r_off[s] : r_off[s] + ROWS * r],
                in_=rm.rearrange("(q t) d -> q (t d)", t=ROWS),
            )
        for s, (lm, rm, np_, r) in enumerate(terms):
            nc.sync.dma_start(
                out=raw[l_base[s] : l_base[s] + np_, r_cols + l_off[s] : r_cols + l_off[s] + np_], in_=lm
            )
        nc.vector.memset(rawb[:].bitcast(F32), 0.0)
        nc.sync.dma_start(out=rawb[3 * SLOT : 3 * SLOT + 1, :], in_=bias.unsqueeze(0))

        for s, (lm, rm, np_, r) in enumerate(terms):
            nq = r // ROWS
            rows = slice(SLOT * s, SLOT * s + SLOT)
            nc.vector.tensor_copy(
                out=sel1[rows, :].rearrange("k (a b) -> k a b", b=nq),
                in_=ident[rows, SLOT * s : SLOT * s + nq].unsqueeze(1).to_broadcast([SLOT, P // nq, nq]),
            )
            n_rows = max(np_, SLOT)
            rows = slice(l_base[s], l_base[s] + n_rows)
            nc.vector.tensor_copy(
                out=sel2[rows, :].rearrange("k (a b) -> k a b", b=nq),
                in_=ident[rows, l_base[s] : l_base[s] + np_].unsqueeze(2).to_broadcast([n_rows, np_, nq]),
            )
        nc.vector.tensor_copy(
            out=sel1[3 * SLOT : P, :], in_=ident[3 * SLOT : P, 3 * SLOT : 3 * SLOT + 1].to_broadcast([SLOT, P])
        )

        def select_r(bank, lo, s):
            w = PACK * terms[s][3]
            for g in range(PASSES):
                nc.tensor.matmul(
                    out=bank[:, lo + w * g : lo + w * (g + 1)].rearrange("p (d t) -> p d t", t=PACK),
                    lhsT=sel1[:],
                    rhs=raw[:, r_off[s] + w * g : r_off[s] + w * (g + 1)].rearrange("k (t d) -> k d t", t=PACK),
                    start=True,
                    stop=True,
                )

        bank_r1 = psum.tile([P, HALF], F32, tag="bank")
        select_r(bank_r1, 0, 0)
        bank_l = psum.tile([P, HALF], F32, tag="bank")
        nc.tensor.matmul(
            out=bank_l[:, 0:l_pad], lhsT=sel2[:], rhs=raw[:, r_cols : r_cols + l_pad], start=True, stop=True
        )
        bank_r = psum_r.tile([P, HALF], F32)
        for s in range(1, len(terms)):
            select_r(bank_r, r_off[s] - r1_cols, s)
        nc.vector.tensor_scalar(
            out=lrow[:], in0=bank_l[:, 0:l_cols], scalar1=1.0 / 3.0, scalar2=None, op0=MULT
        )
        nc.scalar.copy(out=rrow1[:], in_=bank_r1[:])
        for h in range(2):
            bank_b = psum.tile([P, HALF], F32, tag="bank")
            nc.tensor.matmul(
                out=bank_b[:], lhsT=sel1[:], rhs=rawb[:, HALF * h : HALF * h + HALF], start=True, stop=True
            )
            nc.scalar.copy(out=bias_sb[:, HALF * h : HALF * h + HALF], in_=bank_b[:])

        def x_transpose(m):
            xw = x_raw[m][:].bitcast(F32)
            xgw = xg[:, X_COLS * m : X_COLS * m + X_COLS].bitcast(F32)
            for j in range(J):
                xt = psum.tile([P, 2 * PASSES, P], F32, tag="bank")
                words = xw[:, HALF * j : HALF * j + HALF].rearrange("m (p q) -> m q p", q=2 * PASSES)
                for q in range(2 * PASSES):
                    nc.tensor.transpose(xt[:, q, :], words[:, q, :], ident[:])
                nc.scalar.copy(
                    out=xgw[:, HALF * j : HALF * j + HALF].rearrange("p (g m u) -> p g m u", g=PASSES, u=2),
                    in_=xt[:].rearrange("p (g u) m -> p g m u", u=2),
                )

        def x_quant(c):
            nc.vector.quantize_mx(
                out=xc[:, PAIR * X_WORDS * c : PAIR * X_WORDS * (c + 1)].bitcast(FP8X4),
                scales=xs[:, PAIR * X_WORDS * c : PAIR * X_WORDS * (c + 1)],
                in_=xg[:, PAIR * X_COLS * c : PAIR * X_COLS * (c + 1)],
            )

        def product(m, j, h):
            pb = psum.tile([P, HALF], F32, tag="bank")
            for g in range(PASSES):
                lo = X_WORDS * m + PASSES * P * j + P * g
                nc.tensor.matmul_mx(
                    out=pb[:],
                    lhsT=xc[:, lo : lo + P].bitcast(FP8X4),
                    lhsT_scale=xs[:, lo : lo + P],
                    rhs=wc[:, g, HALF * h : HALF * h + HALF].bitcast(FP8X4),
                    rhs_scale=ws[:, g, HALF * h : HALF * h + HALF],
                    start=(g == 0),
                    stop=(g == PASSES - 1),
                )
            return pb

        def leave(pb, dst, h, by_scalar):
            bs = bias_sb[:, HALF * h : HALF * h + HALF]
            if by_scalar:
                nc.scalar.copy(out=dst, in_=pb[:])
                nc.gpsimd.tensor_tensor(out=dst, in0=dst, in1=bs, op=ADD)
            else:
                nc.vector.tensor_tensor(out=dst, in0=pb[:], in1=bs, op=ADD)

        late_stores = []

        def half_rows(pool, tag, m, h, n_scalar, store_later=False):
            oh = pool.tile([P, J, HALF], F32, tag=tag, name=tag)
            if n_scalar == J:
                for j in range(J):
                    nc.scalar.copy(out=oh[:, j, :], in_=product(m, j, h)[:])
                bs = bias_sb[:, HALF * h : HALF * h + HALF].unsqueeze(1).to_broadcast([P, J, HALF])
                nc.gpsimd.tensor_tensor(out=oh[:], in0=oh[:], in1=bs, op=ADD)
            else:
                for j in range(J):
                    leave(product(m, j, h), oh[:, j, :], h, j < n_scalar)
            if store_later:
                late_stores.append((m, h, oh))
            else:
                nc.sync.dma_start(out=ov[m][:, :, HALF * h : HALF * h + HALF], in_=oh[:])

        def store_late():
            m, h, oh = late_stores.pop(0)
            nc.sync.dma_start(out=ov[m][:, :, HALF * h : HALF * h + HALF], in_=oh[:])

        for m in range(FIRST_T):
            x_load(m)
            x_transpose(m)

        with tc.tile_pool(name="wpool", bufs=1) as wpool:
            w1 = PACK * terms[0][3]
            acc = wpool.tile([P, terms[0][2], PASSES, w1], F32)
            wbf = wpool.tile([P, PASSES, PACK * D], BF16, align_bytes=64)

            def w_term(s, h, first=0, last=None, on_gpsimd=False):
                lm, rm, np_, r = terms[s]
                w = PACK * r
                row1 = rrow1[:].rearrange("p (g c) -> p g c", g=PASSES)
                for b in list(range(h * np_ // 2, (h + 1) * np_ // 2))[first:last]:
                    sc = lrow[:, l_off[s] + b : l_off[s] + b + 1]
                    dst = acc[:, w * b // w1, :, w * b % w1 : w * b % w1 + w]
                    if s == 0 and on_gpsimd:
                        nc.gpsimd.tensor_scalar(out=dst, in0=row1, scalar1=sc, scalar2=0.0, op0=MULT, op1=ADD)
                    elif s == 0:
                        nc.vector.tensor_scalar(out=dst, in0=row1, scalar1=sc, scalar2=None, op0=MULT)
                    else:
                        res = dst if s == 1 else wbf[:, :, w * b : w * b + w]
                        lo = r_off[s] - r1_cols
                        nc.vector.scalar_tensor_tensor(
                            out=res,
                            in0=bank_r[:, lo : lo + ROWS * r].rearrange("p (g c) -> p g c", g=PASSES),
                            scalar=sc,
                            in1=dst,
                            op0=MULT,
                            op1=ADD,
                        )

            def w_quant(g, lo, n):
                nc.vector.quantize_mx(
                    out=wc[:, g, lo : lo + n].bitcast(FP8X4),
                    scales=ws[:, g, lo : lo + n],
                    in_=wbf[:, g, PACK * lo : PACK * (lo + n)],
                )

            w_term(0, 0, last=V_FIRST)
            w_term(0, 0, first=V_FIRST, on_gpsimd=True)
            w_term(0, 1, on_gpsimd=True)

            def w_rest(h, lo, hi):
                for s in range(1, len(terms)):
                    per = terms[s][2] // terms[0][2]
                    w_term(s, h, first=per * lo, last=per * hi)

            for lo in range(0, N_BLOCKS, 2):
                w_rest(0, lo, lo + 2)
            w_rest(1, 0, 1)
            for g in range(PASSES):
                w_quant(g, 0, HALF)
            x_quant(0)
            x_quant(1)
            x_quant(2)
            for m in range(FIRST_T, N_MACRO):
                x_load(m)

            def early(e):
                half_rows(hpool, "oh", e, 0, J, store_later=e >= LATE_FROM)

            early(0)
            x_transpose(12)
            early(1)
            x_transpose(13)
            w_rest(1, 1, 3)
            early(2)
            x_transpose(14)
            early(3)
            x_transpose(15)
            w_rest(1, 3, 6)
            early(4)
            early(5)
            w_rest(1, 6, N_BLOCKS)
            for lo in (HALF, HALF + HALF // 2):
                for g in range(PASSES):
                    w_quant(g, lo, HALF // 2)

        opool = ctx.enter_context(tc.tile_pool(name="opool", bufs=6))
        for m in range(N_MACRO):
            c = (m + QUANT_LEAD) // PAIR
            if (m + QUANT_LEAD) % PAIR == 0 and (EARLY + 1) // PAIR <= c < N_MACRO // PAIR:
                x_quant(c)
            if m < EARLY:
                half_rows(opool, "ot", m, 1, R_SCALAR[m])
                if m in LATE_AFTER:
                    store_late()
                continue
            last = m == N_MACRO - 1
            ot = opool.tile([P, J, D], F32, tag="ot")
            for j in range(J):
                for h in range(2):
                    by_scalar = j == 0 and h == 0 and not last
                    leave(product(m, j, h), ot[:, j, HALF * h : HALF * h + HALF], h, by_scalar)
                if last:
                    nc.sync.dma_start(out=ov[m][:, j, :], in_=ot[:, j, :])
            if not last:
                nc.sync.dma_start(out=ov[m], in_=ot[:])
